import numpy as np
import ml_dtypes


def mxq(x, axis, fmt="e4m3"):
    dtype, down = {"e4m3": (ml_dtypes.float8_e4m3fn, 7), "e5m2": (ml_dtypes.float8_e5m2, 14)}[fmt]
    v = np.moveaxis(np.asarray(x, np.float32).astype(ml_dtypes.bfloat16).astype(np.float64), axis, -1)
    blocks = v.reshape(v.shape[:-1] + (-1, 32))
    amax = np.abs(blocks).max(-1, keepdims=True)
    byte = np.maximum(np.where(amax > 0, np.frexp(amax)[1] - 1 + 127, 0) - down, 1)
    scale = np.exp2(byte - 127.0)
    codes = (blocks / scale).astype(np.float32).astype(dtype).astype(np.float64)
    return np.moveaxis((codes * scale).reshape(v.shape), -1, axis)


WIDE = False


def mx_kscale(k):
    if not WIDE:
        return np.ones(k)
    levels = np.array([10, -10, 5, -5, 0])
    if k % 512:
        return np.exp2(np.random.permutation(np.resize(levels, k // 32))).repeat(32)
    a = np.empty((k // 512, 16))
    for p in range(k // 512):
        a[p, :8] = np.random.permutation(np.resize(levels, 8))
        for g in range(8):
            far = levels[np.abs(levels - a[p, g]) >= 10]
            a[p, g + 8] = far[np.random.randint(len(far))]
    return np.exp2(a.ravel()).repeat(32)


BF16 = ml_dtypes.bfloat16


def bf(x):
    return np.asarray(x, np.float32).astype(BF16)


def f64(x):
    return np.asarray(x).astype(np.float64)


E2M1 = np.array([0.0, 0.5, 1.0, 1.5, 2.0, 3.0, 4.0, 6.0, -0.0, -0.5, -1.0, -1.5, -2.0, -3.0, -4.0, -6.0])


def pack_weight(w, fmt):
    k, n = w.shape
    w = f64(bf(w)).reshape(k // 32, 32, n)
    amax = np.abs(w).max(1)
    if fmt == "e4m3":
        byte = np.frexp(amax)[1] - 1 + 127 - 7
    else:
        mant, ex = np.frexp(amax / 6.0)
        byte = np.where(mant > 0.5, ex, ex - 1) + 127
    byte = np.clip(np.where(amax > 0, byte, 1), 1, 254)
    scaled = (w * np.exp2(127.0 - byte)[:, None, :]).reshape(k, n).astype(np.float32)
    by_word = np.ascontiguousarray(scaled.reshape(k // 512, 128, 4, n).transpose(0, 1, 3, 2))
    if fmt == "e4m3":
        words = by_word.astype(ml_dtypes.float8_e4m3fn).view(np.uint8)
    else:
        c = by_word.astype(ml_dtypes.float4_e2m1fn).view(np.uint8) & 0xF
        words = c[..., 0::2] | (c[..., 1::2] << 4)
    return np.ascontiguousarray(words), np.ascontiguousarray(byte.astype(np.uint8).reshape(k // 512, 16, n))


def unpack_weight(words, scales, fmt):
    g, p, n, _ = words.shape
    if fmt == "e4m3":
        vals = np.ascontiguousarray(words).view(ml_dtypes.float8_e4m3fn).astype(np.float64)
    else:
        nib = np.empty((g, p, n, 4), np.uint8)
        nib[..., 0::2] = words & 0xF
        nib[..., 1::2] = words >> 4
        vals = E2M1[nib]
    vals = vals * np.repeat(np.exp2(scales.astype(np.float64) - 127.0), 8, axis=1)[..., None]
    return vals.transpose(0, 1, 3, 2).reshape(g * 512, n)


B, S, D = 1, 1024, 1024


def sigmoid(z):
    return 1.0 / (1.0 + np.exp(-z))


def draw0():
    s, t = mx_kscale(D), mx_kscale(D)
    x = bf(np.random.standard_normal((B, S, D)) * s)
    wq_w_words, wq_w_scales = pack_weight((np.random.standard_normal((D, D)) / np.sqrt(D) / s).T, 'e4m3')
    wq_b = bf(np.random.standard_normal(D) * 0.1)
    r_aft = bf(np.random.standard_normal((B, S, D)) * 6.0 / np.sqrt(S) * t)
    out_w_words, out_w_scales = pack_weight((np.random.standard_normal((D, D)) * 6.0 / np.sqrt(D) / t).T, 'e4m3')
    out_b = bf(np.random.standard_normal(D) * 0.1)
    return {
        'x': x,
        'wq_w_words': wq_w_words,
        'wq_w_scales': wq_w_scales,
        'wq_b': wq_b,
        'r_aft': r_aft,
        'out_w_words': out_w_words,
        'out_w_scales': out_w_scales,
        'out_b': out_b,
    }


def core(x, wq_w_words, wq_w_scales, wq_b, r_aft, out_w_words, out_w_scales, out_b):
    q = (mxq(f64(x), 2, 'e4m3') @ unpack_weight(wq_w_words, wq_w_scales, 'e4m3')) + f64(wq_b)
    y = sigmoid(q) * f64(r_aft)
    return (mxq(y, 2, 'e4m3') @ unpack_weight(out_w_words, out_w_scales, 'e4m3')) + f64(out_b)


def e4m3fn_bytes(y):
    return np.clip(np.asarray(y, np.float64), -448.0, 448.0).astype(np.float32).astype(ml_dtypes.float8_e4m3fn).view(np.uint8)


def e4m3fn_values(b):
    return np.asarray(b, np.uint8).view(ml_dtypes.float8_e4m3fn).astype(np.float64)


def setup_inputs():
    d = draw0()
    x0 = np.asarray(d['x']).astype(np.float64)
    s = (np.max(np.abs(x0), axis=(0, 1), keepdims=True) / 448.0).astype(np.float32)
    out = {}
    for k, v in d.items():
        if k == 'x':
            out['x_bytes'] = e4m3fn_bytes(x0 / s.astype(np.float64))
            out['x_scale'] = s
        else:
            out[k] = v
    return out


def reference(x_bytes, x_scale, wq_w_words, wq_w_scales, wq_b, r_aft, out_w_words, out_w_scales, out_b):
    return core(e4m3fn_values(x_bytes) * x_scale.astype(np.float64), wq_w_words, wq_w_scales, wq_b, r_aft, out_w_words, out_w_scales, out_b)

@@ -1,0 +1,351 @@
+from contextlib import ExitStack
+
+import concourse.mybir as mybir
+from concourse.masks import make_identity
+
+F32 = mybir.dt.float32
+BF16 = mybir.dt.bfloat16
+I32 = mybir.dt.int32
+U32 = mybir.dt.uint32
+U8 = mybir.dt.uint8
+FP8 = mybir.dt.float8_e4m3fn
+FP8X4 = mybir.dt.float8_e4m3fn_x4
+ACT = mybir.ActivationFunctionType
+ALU = mybir.AluOpType
+
+S, D = 1024, 1024
+P = 128
+G = D // 512
+CH = 256
+NC = S // CH
+FLOPS = 2 * 2 * S * D * D
+
+
+def tile_aft_full_pb_w8_kernel(
+    tc, x_bytes, x_scale, wq_w_words, wq_w_scales, wq_b, r_aft, out_w_words, out_w_scales, out_b, out
+):
+    nc = tc.nc
+    with ExitStack() as ctx:
+        const = ctx.enter_context(tc.tile_pool(name="const", bufs=1))
+        xin = ctx.enter_context(tc.tile_pool(name="xin", bufs=4))
+        rin = ctx.enter_context(tc.tile_pool(name="rin", bufs=4))
+        work = ctx.enter_context(tc.tile_pool(name="work", bufs=3))
+        pst = ctx.enter_context(tc.psum_pool(name="pst", bufs=1))
+        psq = ctx.enter_context(tc.psum_pool(name="psq", bufs=2))
+
+
+        x_view = x_bytes.rearrange("o (p j) k -> p (o j) k", j=8)
+        r_view = r_aft.rearrange("o (p j) k -> p (o j) k", j=8)
+        o_view = out.rearrange("o (p j) k -> p (o j) k", j=8)
+
+        ident = const.tile([P, P], F32, name="ident")
+        warm = const.tile([P, 1], F32, name="warm")
+        ones = const.tile([P, P], BF16, name="ones")
+        b2row = const.tile([P, D], BF16, name="b2row")
+        b2 = const.tile([P, D], F32, name="b2")
+        sx = const.tile([P, G, 4], F32, name="sx")
+        bq = const.tile([P, G, 4], BF16, name="bq")
+        w_raw = const.tile([P, G, D], I32, name="w_raw", align_bytes=64)
+        w_per = const.tile([P, G, D], I32, name="w_per", align_bytes=64)
+        w_out = const.tile([P, G, D], I32, name="w_out", align_bytes=64)
+        ws_raw = const.tile([P, D], U8, name="ws_raw", align_bytes=64)
+        ws_per = const.tile([P, D], U8, name="ws_per", align_bytes=64)
+        ws_out = const.tile([P, D], U8, name="ws_out", align_bytes=64)
+
+        nc.gpsimd.memset(warm[:], 0.0)
+        make_identity(nc, ident[:])
+        nc.gpsimd.memset(ones[:], 1.0)
+        nc.vector.memset(ws_raw[:].bitcast(I32), 0)
+        nc.vector.memset(b2row[:], 0.0)
+        nc.vector.memset(ws_out[:].bitcast(I32), 0)
+        nc.scalar.dma_start(out=sx[:], in_=x_scale.rearrange("o s (g p t) -> p (o s g) t", p=P, t=4))
+        nc.scalar.dma_start(out=bq[:], in_=wq_b.rearrange("(g p t) -> p g t", p=P, t=4))
+        nc.scalar.activation(out=warm[:], in_=warm[:], func=ACT.Sigmoid)
+
+        xb = []
+        rt = []
+
+        def load_x(c, parts=1):
+            t = xin.tile([P, 2, D], U8, name="xbytes")
+            for h in range(parts):
+                lo, hi = h * 2 // parts, (h + 1) * 2 // parts
+                nc.sync.dma_start(out=t[:, lo:hi, :], in_=x_view[:, 2 * c + lo : 2 * c + hi, :])
+            xb.append(t)
+
+        def load_r(c):
+            t = rin.tile([P, 2, D], BF16, name="rrows")
+            nc.sync.dma_start(out=t[:], in_=r_view[:, 2 * c : 2 * c + 2, :])
+            rt.append(t)
+
+        def load_scales(dst, src):
+            for qd in range(4):
+                nc.sync.dma_start(
+                    out=dst[32 * qd : 32 * qd + 4 * G, :].bitcast(I32),
+                    in_=src[:, 4 * qd : 4 * qd + 4, :].bitcast(I32),
+                )
+
+        def load_words(dst, src, g):
+            nc.sync.dma_start(out=dst[:, g, :], in_=src[g].rearrange("p n t -> p (n t)").bitcast(I32))
+
+        load_x(0, 2)
+        load_scales(ws_raw, wq_w_scales)
+        load_words(w_raw, wq_w_words, 0)
+        load_words(w_raw, wq_w_words, 1)
+        load_x(1)
+        nc.sync.dma_start(out=b2row[0:1, :], in_=out_b.rearrange("(o n) -> o n", o=1))
+        load_r(0)
+        load_x(2)
+        load_scales(ws_out, out_w_scales)
+        load_words(w_out, out_w_words, 0)
+        load_words(w_out, out_w_words, 1)
+        load_x(3)
+        load_r(1)
+        load_r(2)
+        load_r(3)
+
+        xw = {}
+        xt = {}
+        xg = {}
+        xc = {}
+        sg = {}
+        rp = {}
+        rs = {}
+        yg = {}
+        yc = {}
+        ob = {}
+        acc = {}
+        raw = {}
+
+        def widen(c, i, eng, lo=0, hi=D):
+            if c not in xw:
+                xw[c] = work.tile([P, 2, D], BF16, name="xw")
+            if eng == "v":
+                nc.vector.tensor_copy(out=xw[c][:, i, lo:hi], in_=xb[c][:, i, lo:hi].bitcast(FP8))
+            else:
+                nc.scalar.copy(out=xw[c][:, i, lo:hi], in_=xb[c][:, i, lo:hi].bitcast(FP8))
+
+        def turn(words, bank, g):
+            for i in range(2):
+                for u in range(2):
+                    nc.tensor.transpose(
+                        bank[:, u, i * P : (i + 1) * P], words[:, i, 256 * g + u : 256 * (g + 1) : 2], ident[:]
+                    )
+
+        def turn_x(c, g):
+            xt[c, g] = pst.tile([P, 2, CH], F32, name="xt" + str(g))
+            turn(xw[c][:].bitcast(F32), xt[c, g], g)
+
+        def sort_r(c, i):
+            if c not in rs:
+                rs[c] = work.tile([P, 2, G, 2, P], F32, name="rsort")
+            nc.scalar.copy(
+                out=rs[c][:, i, :, :, :],
+                in_=rt[c][:, i, :].bitcast(F32).rearrange("p (h m u) -> p h u m", h=G, u=2),
+            )
+
+        def turn_r(c, h):
+            if h == 0:
+                sort_r(c, 0)
+                sort_r(c, 1)
+            rp[c, h] = pst.tile([P, 2, CH], F32, name="rp" + str(h))
+            for i in range(2):
+                for u in range(2):
+                    nc.tensor.transpose(rp[c, h][:, u, i * P : (i + 1) * P], rs[c][:, i, h, u, :], ident[:])
+
+        def halves(bank):
+            return bank[:].rearrange("p u n -> p (u n)").bitcast(BF16).rearrange("p (u n e) -> p n u e", u=2, e=2)
+
+        def product(c, g):
+            if g == 0:
+                xg[c] = work.tile([P, G, CH, 4], BF16, name="xg", align_bytes=64)
+            nc.vector.tensor_tensor(
+                out=xg[c][:, g, :, :].rearrange("p n (u e) -> p n u e", u=2),
+                in0=halves(xt[c, g]),
+                in1=sx[:, g, :].unsqueeze(1).to_broadcast([P, CH, 4]).rearrange("p n (u e) -> p n u e", u=2),
+                op=ALU.mult,
+            )
+
+        def quantise(src, dst, lo, hi):
+            nc.vector.quantize_mx(
+                out=dst[0][:, lo:hi, :].rearrange("p g n -> p (g n)").bitcast(FP8X4),
+                scales=dst[1][:, lo:hi, :].rearrange("p g n -> p (g n)"),
+                in_=src[:, lo:hi, :, :].rearrange("p g n t -> p (g n t)"),
+            )
+
+        def quant_x(c, lo, hi):
+            if lo == 0:
+                xc[c] = (
+                    work.tile([P, G, CH], U32, name="xcodes", align_bytes=64),
+                    work.tile([P, G, CH], U8, name="xcs", align_bytes=64),
+                )
+            quantise(xg[c], xc[c], lo, hi)
+
+        def stage1(c, h):
+            sg[c, h] = work.tile([P, 4, CH], F32, name="sig" + str(h), align_bytes=64)
+            for b in range(2):
+                q = psq.tile([P, 2, CH], F32, name="q")
+                for tt in range(2):
+                    t = 2 * b + tt
+                    cols = slice(512 * h + P * t, 512 * h + P * (t + 1))
+                    for g in range(G):
+                        nc.tensor.matmul_mx(
+                            out=q[:, tt, :],
+                            lhsT=w_per[:, g, cols].bitcast(FP8X4),
+                            lhsT_scale=ws_per[4 * g :, cols],
+                            rhs=xc[c][0][:, g, :].bitcast(FP8X4),
+                            rhs_scale=xc[c][1][:, g, :],
+                            start=(g == 0),
+                            stop=(g == G - 1),
+                        )
+                for tt in range(2):
+                    t = 2 * b + tt
+                    nc.scalar.activation(
+                        out=sg[c, h][:, t, :], in_=q[:, tt, :], func=ACT.Sigmoid, bias=bq[:, h, t : t + 1]
+                    )
+
+        def gate(c, h):
+            if h == 0:
+                yg[c] = work.tile([P, G, CH, 4], BF16, name="yg", align_bytes=64)
+            nc.vector.tensor_tensor(
+                out=yg[c][:, h, :, :].rearrange("p n (u e) -> p n u e", u=2),
+                in0=sg[c, h][:].rearrange("p (u e) n -> p n u e", u=2),
+                in1=halves(rp[c, h]),
+                op=ALU.mult,
+            )
+
+        def quant_y(c, lo, hi):
+            if lo == 0:
+                yc[c] = (
+                    work.tile([P, G, CH], U32, name="ycodes", align_bytes=64),
+                    work.tile([P, G, CH], U8, name="ycs", align_bytes=64),
+                )
+            quantise(yg[c], yc[c], lo, hi)
+
+        def stage2(c, b, hs=(0, 1), bank="o"):
+            i, d = b // 2, b % 2
+            if hs[0] == 0:
+                acc[c, b] = (psq if bank == "o" else pst).tile([P, 512], F32, name=bank)
+            cols = slice(512 * d, 512 * (d + 1))
+            toks = slice(P * i, P * (i + 1))
+            for h in hs:
+                nc.tensor.matmul_mx(
+                    out=acc[c, b][:],
+                    lhsT=yc[c][0][:, h, toks].bitcast(FP8X4),
+                    lhsT_scale=yc[c][1][:, h, toks],
+                    rhs=w_out[:, h, cols].bitcast(FP8X4),
+                    rhs_scale=ws_out[4 * h :, cols],
+                    start=(h == 0),
+                    stop=(h == G - 1),
+                )
+
+        def finish(c, b, how="v"):
+            i, d = b // 2, b % 2
+            cols = slice(512 * d, 512 * (d + 1))
+            if (c, i) not in ob:
+                ob[c, i] = work.tile([P, D], F32, name="ob")
+            if how == "v":
+                nc.vector.tensor_tensor(out=ob[c, i][:, cols], in0=acc[c, b][:], in1=b2[:, cols], op=ALU.add)
+            elif how == "s":
+                raw[c, b] = work.tile([P, 512], F32, name="raw")
+                nc.scalar.copy(out=raw[c, b][:], in_=acc[c, b][:])
+                return
+            else:
+                nc.gpsimd.tensor_tensor(out=ob[c, i][:, cols], in0=raw[c, b][:], in1=b2[:, cols], op=ALU.add)
+            if c == NC - 1:
+                nc.sync.dma_start(out=o_view[:, 2 * c + i, cols], in_=ob[c, i][:, cols])
+            elif d == 1:
+                nc.sync.dma_start(out=o_view[:, 2 * c + i, :], in_=ob[c, i][:])
+
+        def permute(g):
+            nc.vector.tensor_copy(
+                out=w_per[:, g, :].rearrange("p (h t m) -> p h t m", h=2, t=4),
+                in_=w_raw[:, g, :].rearrange("p (h m t) -> p h t m", h=2, t=4),
+            )
+
+        nc.gpsimd.tensor_copy(
+            out=ws_per[:].rearrange("p (h t m) -> p h t m", h=2, t=4),
+            in_=ws_raw[:].rearrange("p (h m t) -> p h t m", h=2, t=4),
+        )
+        widen(0, 0, "s", 0, 512)
+        widen(0, 1, "v", 0, 512)
+        turn_x(0, 0)
+        widen(0, 0, "s", 512, D)
+        widen(0, 1, "v", 512, D)
+        turn_x(0, 1)
+        permute(0)
+        product(0, 0)
+        permute(1)
+        product(0, 1)
+        widen(1, 0, "s")
+        widen(1, 1, "s")
+        turn_x(1, 0)
+        turn_x(1, 1)
+        for d in range(2):
+            cols = slice(512 * d, 512 * (d + 1))
+            bb = psq.tile([P, 512], F32, name="o")
+            nc.tensor.matmul(out=bb[:], lhsT=ones[:], rhs=b2row[:, cols], start=True, stop=True)
+            nc.scalar.copy(out=b2[:, cols], in_=bb[:])
+        quant_x(0, 0, 1)
+        quant_x(0, 1, 2)
+        turn_r(0, 0)
+        turn_r(0, 1)
+        stage1(0, 0)
+        product(1, 0)
+        product(1, 1)
+        stage1(0, 1)
+        quant_x(1, 0, 2)
+        widen(2, 0, "s")
+        widen(2, 1, "s")
+        turn_x(2, 0)
+        turn_x(2, 1)
+
+        for c in range(NC):
+            if c + 1 < NC:
+                stage1(c + 1, 0)
+            if c > 1:
+                finish(c - 2, 2, "g")
+                finish(c - 2, 3, "g")
+            if c + 2 < NC:
+                product(c + 2, 0)
+            gate(c, 0)
+            if c + 1 < NC:
+                stage1(c + 1, 1)
+            if c > 0:
+                stage2(c - 1, 0)
+                stage2(c - 1, 1)
+            if c + 2 < NC:
+                product(c + 2, 1)
+            gate(c, 1)
+            if c + 3 < NC:
+                widen(c + 3, 0, "s")
+                widen(c + 3, 1, "s")
+                turn_x(c + 3, 0)
+                turn_x(c + 3, 1)
+            if c + 1 < NC:
+                turn_r(c + 1, 0)
+                turn_r(c + 1, 1)
+            if c > 0:
+                finish(c - 1, 0)
+                finish(c - 1, 1)
+                stage2(c - 1, 2)
+                stage2(c - 1, 3)
+                finish(c - 1, 2, "s")
+                finish(c - 1, 3, "s")
+            if c + 2 < NC:
+                quant_x(c + 2, 0, 2)
+            if c < NC - 1:
+                quant_y(c, 0, 2)
+            else:
+                quant_y(c, 0, 1)
+                for b in range(4):
+                    stage2(c, b, (0,), ("o", "o", "xt0", "xt1")[b])
+                quant_y(c, 1, 2)
+        finish(NC - 2, 2, "g")
+        finish(NC - 2, 3, "g")
+        for b in range(4):
+            stage2(NC - 1, b, (1,))
+            if b == 0:
+                finish(NC - 1, 0, "s")
+                finish(NC - 1, 0, "g")
+            else:
+                finish(NC - 1, b)

@@ -33,6 +33,7 @@ def tile_aft_full_pb_w8_kernel(
         pst = ctx.enter_context(tc.psum_pool(name="pst", bufs=1))
         psq = ctx.enter_context(tc.psum_pool(name="psq", bufs=2))
 
+        ctx.enter_context(tc.manual_schedule())
 
         x_view = x_bytes.rearrange("o (p j) k -> p (o j) k", j=8)
         r_view = r_aft.rearrange("o (p j) k -> p (o j) k", j=8)
@@ -55,11 +56,12 @@ def tile_aft_full_pb_w8_kernel(
         nc.gpsimd.memset(warm[:], 0.0)
         make_identity(nc, ident[:])
         nc.gpsimd.memset(ones[:], 1.0)
-        nc.vector.memset(ws_raw[:].bitcast(I32), 0)
         nc.vector.memset(b2row[:], 0.0)
+        nc.vector.memset(ws_raw[:].bitcast(I32), 0)
         nc.vector.memset(ws_out[:].bitcast(I32), 0)
         nc.scalar.dma_start(out=sx[:], in_=x_scale.rearrange("o s (g p t) -> p (o s g) t", p=P, t=4))
         nc.scalar.dma_start(out=bq[:], in_=wq_b.rearrange("(g p t) -> p g t", p=P, t=4))
+        nc.scalar.dma_start(out=b2row[0:1, :], in_=out_b.rearrange("(o n) -> o n", o=1))
         nc.scalar.activation(out=warm[:], in_=warm[:], func=ACT.Sigmoid)
 
         xb = []
@@ -87,19 +89,18 @@ def tile_aft_full_pb_w8_kernel(
         def load_words(dst, src, g):
             nc.sync.dma_start(out=dst[:, g, :], in_=src[g].rearrange("p n t -> p (n t)").bitcast(I32))
 
-        load_x(0, 2)
-        load_scales(ws_raw, wq_w_scales)
+        load_x(0)
         load_words(w_raw, wq_w_words, 0)
-        load_words(w_raw, wq_w_words, 1)
         load_x(1)
-        nc.sync.dma_start(out=b2row[0:1, :], in_=out_b.rearrange("(o n) -> o n", o=1))
+        load_scales(ws_raw, wq_w_scales)
+        load_words(w_raw, wq_w_words, 1)
         load_r(0)
         load_x(2)
         load_scales(ws_out, out_w_scales)
-        load_words(w_out, out_w_words, 0)
-        load_words(w_out, out_w_words, 1)
         load_x(3)
         load_r(1)
+        load_words(w_out, out_w_words, 0)
+        load_words(w_out, out_w_words, 1)
         load_r(2)
         load_r(3)
 
@@ -144,13 +145,14 @@ def tile_aft_full_pb_w8_kernel(
             )
 
         def turn_r(c, h):
-            if h == 0:
-                sort_r(c, 0)
-                sort_r(c, 1)
             rp[c, h] = pst.tile([P, 2, CH], F32, name="rp" + str(h))
             for i in range(2):
                 for u in range(2):
-                    nc.tensor.transpose(rp[c, h][:, u, i * P : (i + 1) * P], rs[c][:, i, h, u, :], ident[:])
+                    if c == 0:
+                        words = rt[c][:, i, :].bitcast(F32)[:, 256 * h + u : 256 * (h + 1) : 2]
+                    else:
+                        words = rs[c][:, i, h, u, :]
+                    nc.tensor.transpose(rp[c, h][:, u, i * P : (i + 1) * P], words, ident[:])
 
         def halves(bank):
             return bank[:].rearrange("p u n -> p (u n)").bitcast(BF16).rearrange("p (u n e) -> p n u e", u=2, e=2)
@@ -242,7 +244,7 @@ def tile_aft_full_pb_w8_kernel(
             i, d = b // 2, b % 2
             cols = slice(512 * d, 512 * (d + 1))
             if (c, i) not in ob:
-                ob[c, i] = work.tile([P, D], F32, name="ob")
+                ob[c, i] = work.tile([P, D], F32, name="ob", bufs=8)
             if how == "v":
                 nc.vector.tensor_tensor(out=ob[c, i][:, cols], in0=acc[c, b][:], in1=b2[:, cols], op=ALU.add)
             elif how == "s":
@@ -256,92 +258,111 @@ def tile_aft_full_pb_w8_kernel(
             elif d == 1:
                 nc.sync.dma_start(out=o_view[:, 2 * c + i, :], in_=ob[c, i][:])
 
+        bias_banks = []
+        for d in range(2):
+            bias_banks.append(psq.tile([P, 512], F32, name="o"))
+            nc.tensor.matmul(
+                out=bias_banks[d][:], lhsT=ones[:], rhs=b2row[:, 512 * d : 512 * (d + 1)], start=True, stop=True
+            )
+
+        def keep_bias():
+            for d in range(2):
+                nc.scalar.copy(out=b2[:, 512 * d : 512 * (d + 1)], in_=bias_banks[d][:])
+
         def permute(g):
             nc.vector.tensor_copy(
                 out=w_per[:, g, :].rearrange("p (h t m) -> p h t m", h=2, t=4),
                 in_=w_raw[:, g, :].rearrange("p (h m t) -> p h t m", h=2, t=4),
             )
 
-        nc.gpsimd.tensor_copy(
+        for g in range(G):
+            widen(0, 0, "s", 512 * g, 512 * (g + 1))
+            widen(0, 1, "v", 512 * g, 512 * (g + 1))
+        turn_x(0, 0)
+        turn_x(0, 1)
+        widen(1, 0, "s")
+        widen(1, 1, "s")
+        product(0, 0)
+        permute(0)
+        product(0, 1)
+        permute(1)
+        nc.vector.tensor_copy(
             out=ws_per[:].rearrange("p (h t m) -> p h t m", h=2, t=4),
             in_=ws_raw[:].rearrange("p (h m t) -> p h t m", h=2, t=4),
         )
-        widen(0, 0, "s", 0, 512)
-        widen(0, 1, "v", 0, 512)
-        turn_x(0, 0)
-        widen(0, 0, "s", 512, D)
-        widen(0, 1, "v", 512, D)
-        turn_x(0, 1)
-        permute(0)
-        product(0, 0)
-        permute(1)
-        product(0, 1)
-        widen(1, 0, "s")
-        widen(1, 1, "s")
+        quant_x(0, 0, 2)
         turn_x(1, 0)
         turn_x(1, 1)
-        for d in range(2):
-            cols = slice(512 * d, 512 * (d + 1))
-            bb = psq.tile([P, 512], F32, name="o")
-            nc.tensor.matmul(out=bb[:], lhsT=ones[:], rhs=b2row[:, cols], start=True, stop=True)
-            nc.scalar.copy(out=b2[:, cols], in_=bb[:])
-        quant_x(0, 0, 1)
-        quant_x(0, 1, 2)
         turn_r(0, 0)
         turn_r(0, 1)
-        stage1(0, 0)
+        widen(2, 0, "s")
         product(1, 0)
         product(1, 1)
+        widen(2, 1, "v")
+        stage1(0, 0)
         stage1(0, 1)
         quant_x(1, 0, 2)
-        widen(2, 0, "s")
-        widen(2, 1, "s")
         turn_x(2, 0)
         turn_x(2, 1)
-
+        widen(3, 0, "s")
         for c in range(NC):
-            if c + 1 < NC:
-                stage1(c + 1, 0)
-            if c > 1:
-                finish(c - 2, 2, "g")
-                finish(c - 2, 3, "g")
+            if c > 0:
+                stage2(c - 1, 0)
+                finish(c - 1, 0, "s")
+                finish(c - 1, 0, "g")
+                stage2(c - 1, 1)
+                finish(c - 1, 1, "s")
+                finish(c - 1, 1, "g")
             if c + 2 < NC:
                 product(c + 2, 0)
             gate(c, 0)
-            if c + 1 < NC:
-                stage1(c + 1, 1)
-            if c > 0:
-                stage2(c - 1, 0)
-                stage2(c - 1, 1)
-            if c + 2 < NC:
-                product(c + 2, 1)
-            gate(c, 1)
-            if c + 3 < NC:
-                widen(c + 3, 0, "s")
-                widen(c + 3, 1, "s")
-                turn_x(c + 3, 0)
-                turn_x(c + 3, 1)
-            if c + 1 < NC:
-                turn_r(c + 1, 0)
-                turn_r(c + 1, 1)
-            if c > 0:
-                finish(c - 1, 0)
-                finish(c - 1, 1)
+            if c >= 2:
                 stage2(c - 1, 2)
                 stage2(c - 1, 3)
-                finish(c - 1, 2, "s")
-                finish(c - 1, 3, "s")
+            if c + 1 < NC:
+                stage1(c + 1, 0)
             if c + 2 < NC:
-                quant_x(c + 2, 0, 2)
-            if c < NC - 1:
-                quant_y(c, 0, 2)
-            else:
+                product(c + 2, 1)
+            if c == NC - 1:
+                finish(c - 1, 2)
                 quant_y(c, 0, 1)
                 for b in range(4):
-                    stage2(c, b, (0,), ("o", "o", "xt0", "xt1")[b])
+                    stage2(c, b, (0,), ("rp0", "xt0", "xt1", "o")[b])
+            gate(c, 1)
+            if c == 2:
+                turn_r(c + 1, 0)
+            if c + 1 < NC:
+                stage1(c + 1, 1)
+                if c == 0:
+                    widen(3, 1, "s")
+            if c < 2:
+                sort_r(c + 1, 0)
+                sort_r(c + 1, 1)
+            if c == 1:
+                sort_r(3, 0)
+                sort_r(3, 1)
+            if c == 0:
+                keep_bias()
+            if c == 1:
+                stage2(c - 1, 2)
+                stage2(c - 1, 3)
+            if c == 1 or c == 2:
+                finish(c - 1, 2)
+                finish(c - 1, 3)
+            if c + 3 < NC:
+                turn_x(c + 3, 0)
+                turn_x(c + 3, 1)
+            if c < 2:
+                turn_r(c + 1, 0)
+            if c < 3:
+                turn_r(c + 1, 1)
+            if c + 2 < NC:
+                quant_x(c + 2, 0, 2)
+            if c + 1 < NC:
+                quant_y(c, 0, 2)
+            else:
                 quant_y(c, 1, 2)
-        finish(NC - 2, 2, "g")
-        finish(NC - 2, 3, "g")
+                finish(c - 1, 3)
         for b in range(4):
             stage2(NC - 1, b, (1,))
             if b == 0:

@@ -29,9 +29,9 @@ def tile_aft_full_pb_w8_kernel(
         const = ctx.enter_context(tc.tile_pool(name="const", bufs=1))
         xin = ctx.enter_context(tc.tile_pool(name="xin", bufs=4))
         rin = ctx.enter_context(tc.tile_pool(name="rin", bufs=4))
-        work = ctx.enter_context(tc.tile_pool(name="work", bufs=3))
+        work = ctx.enter_context(tc.tile_pool(name="work", bufs=4))
         pst = ctx.enter_context(tc.psum_pool(name="pst", bufs=1))
-        psq = ctx.enter_context(tc.psum_pool(name="psq", bufs=2))
+        psq = ctx.enter_context(tc.psum_pool(name="psq", bufs=4))
 
         ctx.enter_context(tc.manual_schedule())
 
@@ -41,9 +41,7 @@ def tile_aft_full_pb_w8_kernel(
 
         ident = const.tile([P, P], F32, name="ident")
         warm = const.tile([P, 1], F32, name="warm")
-        ones = const.tile([P, P], BF16, name="ones")
-        b2row = const.tile([P, D], BF16, name="b2row")
-        b2 = const.tile([P, D], F32, name="b2")
+        b2 = const.tile([P, D], BF16, name="b2")
         sx = const.tile([P, G, 4], F32, name="sx")
         bq = const.tile([P, G, 4], BF16, name="bq")
         w_raw = const.tile([P, G, D], I32, name="w_raw", align_bytes=64)
@@ -55,13 +53,10 @@ def tile_aft_full_pb_w8_kernel(
 
         nc.gpsimd.memset(warm[:], 0.0)
         make_identity(nc, ident[:])
-        nc.gpsimd.memset(ones[:], 1.0)
-        nc.vector.memset(b2row[:], 0.0)
         nc.vector.memset(ws_raw[:].bitcast(I32), 0)
         nc.vector.memset(ws_out[:].bitcast(I32), 0)
         nc.scalar.dma_start(out=sx[:], in_=x_scale.rearrange("o s (g p t) -> p (o s g) t", p=P, t=4))
         nc.scalar.dma_start(out=bq[:], in_=wq_b.rearrange("(g p t) -> p g t", p=P, t=4))
-        nc.scalar.dma_start(out=b2row[0:1, :], in_=out_b.rearrange("(o n) -> o n", o=1))
         nc.scalar.activation(out=warm[:], in_=warm[:], func=ACT.Sigmoid)
 
         xb = []
@@ -89,7 +84,7 @@ def tile_aft_full_pb_w8_kernel(
         def load_words(dst, src, g):
             nc.sync.dma_start(out=dst[:, g, :], in_=src[g].rearrange("p n t -> p (n t)").bitcast(I32))
 
-        load_x(0)
+        load_x(0, 2)
         load_words(w_raw, wq_w_words, 0)
         load_x(1)
         load_scales(ws_raw, wq_w_scales)
@@ -97,12 +92,13 @@ def tile_aft_full_pb_w8_kernel(
         load_r(0)
         load_x(2)
         load_scales(ws_out, out_w_scales)
-        load_x(3)
-        load_r(1)
         load_words(w_out, out_w_words, 0)
         load_words(w_out, out_w_words, 1)
+        load_x(3)
+        load_r(1)
         load_r(2)
         load_r(3)
+        nc.sync.dma_start(out=b2[:], in_=out_b.partition_broadcast(P))
 
         xw = {}
         xt = {}
@@ -115,6 +111,7 @@ def tile_aft_full_pb_w8_kernel(
         yc = {}
         ob = {}
         acc = {}
+        acc1 = {}
         raw = {}
 
         def widen(c, i, eng, lo=0, hi=D):
@@ -136,6 +133,12 @@ def tile_aft_full_pb_w8_kernel(
             xt[c, g] = pst.tile([P, 2, CH], F32, name="xt" + str(g))
             turn(xw[c][:].bitcast(F32), xt[c, g], g)
 
+        def turn_first(g, i):
+            xt[0, g, i] = pst.tile([P, 2, P], F32, name="xt" + str(g)) if i == 0 else psq.tile([P, 2, P], F32, name="acc")
+            words = xw[0][:, i, :].bitcast(F32)
+            for u in range(2):
+                nc.tensor.transpose(xt[0, g, i][:, u, :], words[:, 256 * g + u : 256 * (g + 1) : 2], ident[:])
+
         def sort_r(c, i):
             if c not in rs:
                 rs[c] = work.tile([P, 2, G, 2, P], F32, name="rsort")
@@ -148,7 +151,7 @@ def tile_aft_full_pb_w8_kernel(
             rp[c, h] = pst.tile([P, 2, CH], F32, name="rp" + str(h))
             for i in range(2):
                 for u in range(2):
-                    if c == 0:
+                    if c not in rs:
                         words = rt[c][:, i, :].bitcast(F32)[:, 256 * h + u : 256 * (h + 1) : 2]
                     else:
                         words = rs[c][:, i, h, u, :]
@@ -158,12 +161,22 @@ def tile_aft_full_pb_w8_kernel(
             return bank[:].rearrange("p u n -> p (u n)").bitcast(BF16).rearrange("p (u n e) -> p n u e", u=2, e=2)
 
         def product(c, g):
-            if g == 0:
+            if c not in xg:
                 xg[c] = work.tile([P, G, CH, 4], BF16, name="xg", align_bytes=64)
             nc.vector.tensor_tensor(
                 out=xg[c][:, g, :, :].rearrange("p n (u e) -> p n u e", u=2),
                 in0=halves(xt[c, g]),
                 in1=sx[:, g, :].unsqueeze(1).to_broadcast([P, CH, 4]).rearrange("p n (u e) -> p n u e", u=2),
+                op=ALU.mult,
+            )
+
+        def product_first(g, i):
+            if 0 not in xg:
+                xg[0] = work.tile([P, G, CH, 4], BF16, name="xg", align_bytes=64)
+            nc.vector.tensor_tensor(
+                out=xg[0][:, g, i * P : (i + 1) * P, :].rearrange("p n (u e) -> p n u e", u=2),
+                in0=halves(xt[0, g, i]),
+                in1=sx[:, g, :].unsqueeze(1).to_broadcast([P, P, 4]).rearrange("p n (u e) -> p n u e", u=2),
                 op=ALU.mult,
             )
 
@@ -182,31 +195,34 @@ def tile_aft_full_pb_w8_kernel(
                 )
             quantise(xg[c], xc[c], lo, hi)
 
-        def stage1(c, h):
-            sg[c, h] = work.tile([P, 4, CH], F32, name="sig" + str(h), align_bytes=64)
-            for b in range(2):
-                q = psq.tile([P, 2, CH], F32, name="q")
-                for tt in range(2):
-                    t = 2 * b + tt
-                    cols = slice(512 * h + P * t, 512 * h + P * (t + 1))
-                    for g in range(G):
-                        nc.tensor.matmul_mx(
-                            out=q[:, tt, :],
-                            lhsT=w_per[:, g, cols].bitcast(FP8X4),
-                            lhsT_scale=ws_per[4 * g :, cols],
-                            rhs=xc[c][0][:, g, :].bitcast(FP8X4),
-                            rhs_scale=xc[c][1][:, g, :],
-                            start=(g == 0),
-                            stop=(g == G - 1),
-                        )
-                for tt in range(2):
-                    t = 2 * b + tt
-                    nc.scalar.activation(
-                        out=sg[c, h][:, t, :], in_=q[:, tt, :], func=ACT.Sigmoid, bias=bq[:, h, t : t + 1]
+        def stage1(c, h, b):
+            q = psq.tile([P, 2, CH], F32, name="acc")
+            acc1[c, h, b] = q
+            for tt in range(2):
+                t = 2 * b + tt
+                cols = slice(512 * h + P * t, 512 * h + P * (t + 1))
+                for g in range(G):
+                    nc.tensor.matmul_mx(
+                        out=q[:, tt, :],
+                        lhsT=w_per[:, g, cols].bitcast(FP8X4),
+                        lhsT_scale=ws_per[4 * g :, cols],
+                        rhs=xc[c][0][:, g, :].bitcast(FP8X4),
+                        rhs_scale=xc[c][1][:, g, :],
+                        start=(g == 0),
+                        stop=(g == G - 1),
                     )
 
+        def sigmoid(c, h, b):
+            if (c, h) not in sg:
+                sg[c, h] = work.tile([P, 4, CH], F32, name="sig" + str(h), align_bytes=64)
+            for tt in range(2):
+                t = 2 * b + tt
+                nc.scalar.activation(
+                    out=sg[c, h][:, t, :], in_=acc1[c, h, b][:, tt, :], func=ACT.Sigmoid, bias=bq[:, h, t : t + 1]
+                )
+
         def gate(c, h):
-            if h == 0:
+            if c not in yg:
                 yg[c] = work.tile([P, G, CH, 4], BF16, name="yg", align_bytes=64)
             nc.vector.tensor_tensor(
                 out=yg[c][:, h, :, :].rearrange("p n (u e) -> p n u e", u=2),
@@ -216,17 +232,17 @@ def tile_aft_full_pb_w8_kernel(
             )
 
         def quant_y(c, lo, hi):
-            if lo == 0:
+            if c not in yc:
                 yc[c] = (
                     work.tile([P, G, CH], U32, name="ycodes", align_bytes=64),
                     work.tile([P, G, CH], U8, name="ycs", align_bytes=64),
                 )
             quantise(yg[c], yc[c], lo, hi)
 
-        def stage2(c, b, hs=(0, 1), bank="o"):
+        def stage2(c, b, hs=(0, 1)):
             i, d = b // 2, b % 2
             if hs[0] == 0:
-                acc[c, b] = (psq if bank == "o" else pst).tile([P, 512], F32, name=bank)
+                acc[c, b] = psq.tile([P, 512], F32, name="acc")
             cols = slice(512 * d, 512 * (d + 1))
             toks = slice(P * i, P * (i + 1))
             for h in hs:
@@ -253,21 +269,7 @@ def tile_aft_full_pb_w8_kernel(
                 return
             else:
                 nc.gpsimd.tensor_tensor(out=ob[c, i][:, cols], in0=raw[c, b][:], in1=b2[:, cols], op=ALU.add)
-            if c == NC - 1:
-                nc.sync.dma_start(out=o_view[:, 2 * c + i, cols], in_=ob[c, i][:, cols])
-            elif d == 1:
-                nc.sync.dma_start(out=o_view[:, 2 * c + i, :], in_=ob[c, i][:])
-
-        bias_banks = []
-        for d in range(2):
-            bias_banks.append(psq.tile([P, 512], F32, name="o"))
-            nc.tensor.matmul(
-                out=bias_banks[d][:], lhsT=ones[:], rhs=b2row[:, 512 * d : 512 * (d + 1)], start=True, stop=True
-            )
-
-        def keep_bias():
-            for d in range(2):
-                nc.scalar.copy(out=b2[:, 512 * d : 512 * (d + 1)], in_=bias_banks[d][:])
+            nc.sync.dma_start(out=o_view[:, 2 * c + i, cols], in_=ob[c, i][:, cols])
 
         def permute(g):
             nc.vector.tensor_copy(
@@ -275,98 +277,146 @@ def tile_aft_full_pb_w8_kernel(
                 in_=w_raw[:, g, :].rearrange("p (h m t) -> p h t m", h=2, t=4),
             )
 
-        for g in range(G):
-            widen(0, 0, "s", 512 * g, 512 * (g + 1))
-            widen(0, 1, "v", 512 * g, 512 * (g + 1))
-        turn_x(0, 0)
-        turn_x(0, 1)
-        widen(1, 0, "s")
-        widen(1, 1, "s")
-        product(0, 0)
+        def permute_scales(eng):
+            (nc.vector if eng == "V" else nc.gpsimd).tensor_copy(
+                out=ws_per[:].rearrange("p (h t m) -> p h t m", h=2, t=4),
+                in_=ws_raw[:].rearrange("p (h m t) -> p h t m", h=2, t=4),
+            )
+
+        widen(0, 0, "v", 512, 1024)
+        widen(0, 0, "s", 0, 512)
+        widen(0, 1, "v", 512, 1024)
+        widen(0, 1, "s", 0, 512)
+        turn_first(1, 0)
+        turn_first(1, 1)
+        turn_first(0, 0)
         permute(0)
-        product(0, 1)
+        turn_first(0, 1)
+        widen(1, 1, "s")
+        product_first(1, 1)
+        permute_scales("G")
+        product_first(0, 0)
+        widen(1, 0, "s")
+        product_first(1, 0)
+        product_first(0, 1)
         permute(1)
-        nc.vector.tensor_copy(
-            out=ws_per[:].rearrange("p (h t m) -> p h t m", h=2, t=4),
-            in_=ws_raw[:].rearrange("p (h m t) -> p h t m", h=2, t=4),
-        )
-        quant_x(0, 0, 2)
         turn_x(1, 0)
-        turn_x(1, 1)
-        turn_r(0, 0)
-        turn_r(0, 1)
+        quant_x(0, 0, 2)
         widen(2, 0, "s")
+        turn_x(1, 1)
         product(1, 0)
+        stage1(0, 0, 1)
+        widen(2, 1, "s")
+        stage1(0, 0, 0)
         product(1, 1)
-        widen(2, 1, "v")
-        stage1(0, 0)
-        stage1(0, 1)
-        quant_x(1, 0, 2)
+        turn_r(0, 0)
+        sigmoid(0, 0, 0)
         turn_x(2, 0)
+        sigmoid(0, 0, 1)
+        quant_x(1, 0, 2)
         turn_x(2, 1)
+        widen(3, 1, "s")
+        product(2, 0)
+        turn_r(0, 1)
+        stage1(0, 1, 1)
         widen(3, 0, "s")
-        for c in range(NC):
-            if c > 0:
-                stage2(c - 1, 0)
-                finish(c - 1, 0, "s")
-                finish(c - 1, 0, "g")
-                stage2(c - 1, 1)
-                finish(c - 1, 1, "s")
-                finish(c - 1, 1, "g")
-            if c + 2 < NC:
-                product(c + 2, 0)
-            gate(c, 0)
-            if c >= 2:
-                stage2(c - 1, 2)
-                stage2(c - 1, 3)
-            if c + 1 < NC:
-                stage1(c + 1, 0)
-            if c + 2 < NC:
-                product(c + 2, 1)
-            if c == NC - 1:
-                finish(c - 1, 2)
-                quant_y(c, 0, 1)
-                for b in range(4):
-                    stage2(c, b, (0,), ("rp0", "xt0", "xt1", "o")[b])
-            gate(c, 1)
-            if c == 2:
-                turn_r(c + 1, 0)
-            if c + 1 < NC:
-                stage1(c + 1, 1)
-                if c == 0:
-                    widen(3, 1, "s")
-            if c < 2:
-                sort_r(c + 1, 0)
-                sort_r(c + 1, 1)
-            if c == 1:
-                sort_r(3, 0)
-                sort_r(3, 1)
-            if c == 0:
-                keep_bias()
-            if c == 1:
-                stage2(c - 1, 2)
-                stage2(c - 1, 3)
-            if c == 1 or c == 2:
-                finish(c - 1, 2)
-                finish(c - 1, 3)
-            if c + 3 < NC:
-                turn_x(c + 3, 0)
-                turn_x(c + 3, 1)
-            if c < 2:
-                turn_r(c + 1, 0)
-            if c < 3:
-                turn_r(c + 1, 1)
-            if c + 2 < NC:
-                quant_x(c + 2, 0, 2)
-            if c + 1 < NC:
-                quant_y(c, 0, 2)
-            else:
-                quant_y(c, 1, 2)
-                finish(c - 1, 3)
-        for b in range(4):
-            stage2(NC - 1, b, (1,))
-            if b == 0:
-                finish(NC - 1, 0, "s")
-                finish(NC - 1, 0, "g")
-            else:
-                finish(NC - 1, b)
+        product(2, 1)
+        stage1(0, 1, 0)
+        stage1(1, 0, 0)
+        sigmoid(0, 1, 1)
+        gate(0, 0)
+        stage1(1, 1, 1)
+        sigmoid(0, 1, 0)
+        stage1(1, 1, 0)
+        sort_r(2, 0)
+        quant_x(2, 0, 2)
+        sigmoid(1, 0, 0)
+        turn_x(3, 0)
+        gate(0, 1)
+        sigmoid(1, 1, 0)
+        turn_x(3, 1)
+        sort_r(2, 1)
+        turn_r(1, 0)
+        product(3, 0)
+        sigmoid(1, 1, 1)
+        turn_r(1, 1)
+        sort_r(3, 1)
+        stage1(2, 0, 1)
+        quant_y(0, 0, 2)
+        sort_r(3, 0)
+        stage1(2, 0, 0)
+        product(3, 1)
+        sigmoid(2, 0, 1)
+        stage1(1, 0, 1)
+        sigmoid(2, 0, 0)
+        stage1(2, 1, 1)
+        gate(1, 1)
+        sigmoid(1, 0, 1)
+        stage1(2, 1, 0)
+        sigmoid(2, 1, 1)
+        stage2(0, 2)
+        quant_x(3, 0, 2)
+        sigmoid(2, 1, 0)
+        gate(1, 0)
+        turn_r(2, 1)
+        stage1(3, 1, 0)
+        stage1(3, 0, 0)
+        gate(2, 1)
+        sigmoid(3, 1, 0)
+        stage1(3, 1, 1)
+        finish(0, 2, "s")
+        quant_y(1, 0, 2)
+        turn_r(2, 0)
+        sigmoid(3, 1, 1)
+        turn_r(3, 1)
+        finish(0, 2, "g")
+        gate(2, 0)
+        sigmoid(3, 0, 0)
+        stage2(1, 2)
+        stage2(0, 3)
+        gate(3, 1)
+        finish(1, 2, "s")
+        stage2(0, 0)
+        finish(0, 3, "s")
+        stage2(1, 3)
+        finish(1, 2, "g")
+        finish(0, 0, "v")
+        stage1(3, 0, 1)
+        quant_y(3, 1, 2)
+        finish(1, 3, "s")
+        stage2(1, 0)
+        quant_y(2, 0, 2)
+        sigmoid(3, 0, 1)
+        turn_r(3, 0)
+        finish(1, 3, "g")
+        finish(1, 0, "v")
+        stage2(2, 1)
+        gate(3, 0)
+        stage2(2, 2)
+        finish(0, 3, "g")
+        stage2(1, 1)
+        finish(2, 1, "v")
+        finish(2, 2, "s")
+        stage2(2, 3)
+        quant_y(3, 0, 1)
+        finish(1, 1, "v")
+        finish(2, 2, "g")
+        stage2(2, 0)
+        finish(2, 3, "s")
+        stage2(3, 3, (0,))
+        stage2(3, 3, (1,))
+        finish(2, 0, "v")
+        stage2(3, 0, (0,))
+        finish(2, 3, "g")
+        stage2(3, 2, (0,))
+        finish(3, 3, "v")
+        stage2(3, 0, (1,))
+        stage2(3, 2, (1,))
+        stage2(3, 1, (0,))
+        finish(3, 0, "s")
+        stage2(3, 1, (1,))
+        finish(3, 2, "v")
+        stage2(0, 1)
+        finish(3, 1, "v")
+        finish(3, 0, "g")
+        finish(0, 1, "v")

@@ -15,9 +15,14 @@ ALU = mybir.AluOpType
 
 S, D = 1024, 1024
 P = 128
-G = D // 512
-CH = 256
-NC = S // CH
+PACK = 4
+G = D // (P * PACK)
+CHUNKS = 4
+CH = S // CHUNKS
+HALVES = CH // P
+RUN = 4
+N_OUT = 512
+
 FLOPS = 2 * 2 * S * D * D
 
 
@@ -27,396 +32,381 @@ def tile_aft_full_pb_w8_kernel(
     nc = tc.nc
     with ExitStack() as ctx:
         const = ctx.enter_context(tc.tile_pool(name="const", bufs=1))
-        xin = ctx.enter_context(tc.tile_pool(name="xin", bufs=4))
-        rin = ctx.enter_context(tc.tile_pool(name="rin", bufs=4))
-        work = ctx.enter_context(tc.tile_pool(name="work", bufs=4))
-        pst = ctx.enter_context(tc.psum_pool(name="pst", bufs=1))
-        psq = ctx.enter_context(tc.psum_pool(name="psq", bufs=4))
-
+        work = ctx.enter_context(tc.tile_pool(name="work", bufs=CHUNKS))
+        turned = ctx.enter_context(tc.psum_pool(name="turned", bufs=1))
+        sums = ctx.enter_context(tc.psum_pool(name="sums", bufs=4))
         ctx.enter_context(tc.manual_schedule())
 
-        x_view = x_bytes.rearrange("o (p j) k -> p (o j) k", j=8)
-        r_view = r_aft.rearrange("o (p j) k -> p (o j) k", j=8)
-        o_view = out.rearrange("o (p j) k -> p (o j) k", j=8)
+        x_rows = x_bytes.rearrange("o (p j) k -> p (o j) k", j=CHUNKS * HALVES)
+        r_rows = r_aft.rearrange("o (p j) k -> p (o j) k", j=CHUNKS * HALVES)
+        out_rows = out.rearrange("o (p j) k -> p (o j) k", j=CHUNKS * HALVES)
 
         ident = const.tile([P, P], F32, name="ident")
         warm = const.tile([P, 1], F32, name="warm")
-        b2 = const.tile([P, D], BF16, name="b2")
-        sx = const.tile([P, G, 4], F32, name="sx")
-        bq = const.tile([P, G, 4], BF16, name="bq")
-        w_raw = const.tile([P, G, D], I32, name="w_raw", align_bytes=64)
-        w_per = const.tile([P, G, D], I32, name="w_per", align_bytes=64)
-        w_out = const.tile([P, G, D], I32, name="w_out", align_bytes=64)
-        ws_raw = const.tile([P, D], U8, name="ws_raw", align_bytes=64)
-        ws_per = const.tile([P, D], U8, name="ws_per", align_bytes=64)
-        ws_out = const.tile([P, D], U8, name="ws_out", align_bytes=64)
+        scale_x_by = const.tile([P, G, PACK], F32, name="scale_x_by")
+        wq_bias = const.tile([P, G, PACK], BF16, name="wq_bias")
+        out_bias = const.tile([P, D], BF16, name="out_bias")
+        wq_words = const.tile([P, G, D], I32, name="wq_words", align_bytes=64)
+        wq_sorted = const.tile([P, G, D], I32, name="wq_sorted", align_bytes=64)
+        out_words = const.tile([P, G, D], I32, name="out_words", align_bytes=64)
+        wq_planes = const.tile([P, D], U8, name="wq_planes", align_bytes=64)
+        wq_planes_sorted = const.tile([P, D], U8, name="wq_planes_sorted", align_bytes=64)
+        out_planes = const.tile([P, D], U8, name="out_planes", align_bytes=64)
 
         nc.gpsimd.memset(warm[:], 0.0)
         make_identity(nc, ident[:])
-        nc.vector.memset(ws_raw[:].bitcast(I32), 0)
-        nc.vector.memset(ws_out[:].bitcast(I32), 0)
-        nc.scalar.dma_start(out=sx[:], in_=x_scale.rearrange("o s (g p t) -> p (o s g) t", p=P, t=4))
-        nc.scalar.dma_start(out=bq[:], in_=wq_b.rearrange("(g p t) -> p g t", p=P, t=4))
+        nc.vector.memset(wq_planes[:].bitcast(I32), 0)
+        nc.vector.memset(out_planes[:].bitcast(I32), 0)
+        nc.scalar.dma_start(out=scale_x_by[:], in_=x_scale.rearrange("o s (g p t) -> p (o s g) t", p=P, t=PACK))
         nc.scalar.activation(out=warm[:], in_=warm[:], func=ACT.Sigmoid)
 
-        xb = []
-        rt = []
+        x_raw, x_wide, x_turned, x_scaled, x_mx = {}, {}, {}, {}, {}
+        r_raw, r_sorted, r_turned = {}, {}, {}
+        q_sums, sig, y, y_mx = {}, {}, {}, {}
+        out_sums, stashed, result = {}, {}, {}
 
-        def load_x(c, parts=1):
-            t = xin.tile([P, 2, D], U8, name="xbytes")
-            for h in range(parts):
-                lo, hi = h * 2 // parts, (h + 1) * 2 // parts
-                nc.sync.dma_start(out=t[:, lo:hi, :], in_=x_view[:, 2 * c + lo : 2 * c + hi, :])
-            xb.append(t)
+        def load_x(c, lo, hi):
+            if c not in x_raw:
+                x_raw[c] = work.tile([P, HALVES, D], U8, name="x_raw")
+            nc.sync.dma_start(out=x_raw[c][:, lo:hi, :], in_=x_rows[:, HALVES * c + lo : HALVES * c + hi, :])
 
         def load_r(c):
-            t = rin.tile([P, 2, D], BF16, name="rrows")
-            nc.sync.dma_start(out=t[:], in_=r_view[:, 2 * c : 2 * c + 2, :])
-            rt.append(t)
+            r_raw[c] = work.tile([P, HALVES, D], BF16, name="r_raw")
+            nc.sync.dma_start(out=r_raw[c][:], in_=r_rows[:, HALVES * c : HALVES * (c + 1), :])
 
-        def load_scales(dst, src):
-            for qd in range(4):
+        def load_words(words, source, g):
+            nc.sync.dma_start(out=words[:, g, :], in_=source[g].rearrange("p n t -> p (n t)").bitcast(I32))
+
+        def load_scales(planes, source):
+            for quad in range(4):
                 nc.sync.dma_start(
-                    out=dst[32 * qd : 32 * qd + 4 * G, :].bitcast(I32),
-                    in_=src[:, 4 * qd : 4 * qd + 4, :].bitcast(I32),
+                    out=planes[32 * quad : 32 * quad + 4 * G, :].bitcast(I32),
+                    in_=source[:, 4 * quad : 4 * quad + 4, :].bitcast(I32),
                 )
 
-        def load_words(dst, src, g):
-            nc.sync.dma_start(out=dst[:, g, :], in_=src[g].rearrange("p n t -> p (n t)").bitcast(I32))
+        def permute_words(g):
+            nc.vector.tensor_copy(
+                out=wq_sorted[:, g, :].rearrange("p (h t m) -> p h m t", h=G, t=PACK),
+                in_=wq_words[:, g, :].rearrange("p (h m t) -> p h m t", h=G, t=PACK),
+            )
 
-        load_x(0, 2)
-        load_words(w_raw, wq_w_words, 0)
-        load_x(1)
-        load_scales(ws_raw, wq_w_scales)
-        load_words(w_raw, wq_w_words, 1)
-        load_r(0)
-        load_x(2)
-        load_scales(ws_out, out_w_scales)
-        load_words(w_out, out_w_words, 0)
-        load_words(w_out, out_w_words, 1)
-        load_x(3)
-        load_r(1)
-        load_r(2)
-        load_r(3)
-        nc.sync.dma_start(out=b2[:], in_=out_b.partition_broadcast(P))
+        def permute_scales(engine):
+            engine.tensor_copy(
+                out=wq_planes_sorted[:].rearrange("p (h t m) -> p h t m", h=G, t=PACK),
+                in_=wq_planes[:].rearrange("p (h m t) -> p h t m", h=G, t=PACK),
+            )
 
-        xw = {}
-        xt = {}
-        xg = {}
-        xc = {}
-        sg = {}
-        rp = {}
-        rs = {}
-        yg = {}
-        yc = {}
-        ob = {}
-        acc = {}
-        acc1 = {}
-        raw = {}
+        def widen(copy, c, i, cols):
+            if c not in x_wide:
+                x_wide[c] = work.tile([P, HALVES, D], BF16, name="x_wide")
+            copy(out=x_wide[c][:, i, cols], in_=x_raw[c][:, i, cols].bitcast(FP8))
 
-        def widen(c, i, eng, lo=0, hi=D):
-            if c not in xw:
-                xw[c] = work.tile([P, 2, D], BF16, name="xw")
-            if eng == "v":
-                nc.vector.tensor_copy(out=xw[c][:, i, lo:hi], in_=xb[c][:, i, lo:hi].bitcast(FP8))
-            else:
-                nc.scalar.copy(out=xw[c][:, i, lo:hi], in_=xb[c][:, i, lo:hi].bitcast(FP8))
+        def words_of(row_tile, i, group, u):
+            return row_tile[:, i, :].bitcast(F32)[:, 256 * group + u : 256 * (group + 1) : 2]
 
-        def turn(words, bank, g):
-            for i in range(2):
-                for u in range(2):
-                    nc.tensor.transpose(
-                        bank[:, u, i * P : (i + 1) * P], words[:, i, 256 * g + u : 256 * (g + 1) : 2], ident[:]
-                    )
+        def slots_of(bank):
+            return bank[:].rearrange("p u n -> p (u n)").bitcast(BF16).rearrange("p (u n e) -> p n u e", u=2, e=2)
 
         def turn_x(c, g):
-            xt[c, g] = pst.tile([P, 2, CH], F32, name="xt" + str(g))
-            turn(xw[c][:].bitcast(F32), xt[c, g], g)
+            x_turned[c, g] = turned.tile([P, 2, CH], F32, name="x_turned" + str(g))
+            for i in range(HALVES):
+                for u in range(2):
+                    nc.tensor.transpose(
+                        x_turned[c, g][:, u, P * i : P * (i + 1)], words_of(x_wide[c], i, g, u), ident[:]
+                    )
 
-        def turn_first(g, i):
-            xt[0, g, i] = pst.tile([P, 2, P], F32, name="xt" + str(g)) if i == 0 else psq.tile([P, 2, P], F32, name="acc")
-            words = xw[0][:, i, :].bitcast(F32)
+        def scaled(c, g, lo, hi, bank):
+            if c not in x_scaled:
+                x_scaled[c] = work.tile([P, G, CH, PACK], BF16, name="x_scaled", align_bytes=64)
+            by = scale_x_by[:, g, :].unsqueeze(1).to_broadcast([P, hi - lo, PACK])
+            nc.vector.tensor_tensor(
+                out=x_scaled[c][:, g, lo:hi, :].rearrange("p n (u e) -> p n u e", u=2),
+                in0=slots_of(bank),
+                in1=by.rearrange("p n (u e) -> p n u e", u=2),
+                op=ALU.mult,
+            )
+
+        def scale_x(c, g):
+            scaled(c, g, 0, CH, x_turned[c, g])
+
+        def turn_x_half(g, i):
+            if i == 0:
+                x_turned[0, g, i] = turned.tile([P, 2, P], F32, name="x_turned" + str(g))
+            else:
+                x_turned[0, g, i] = sums.tile([P, 2, P], F32, name="bank")
             for u in range(2):
-                nc.tensor.transpose(xt[0, g, i][:, u, :], words[:, 256 * g + u : 256 * (g + 1) : 2], ident[:])
+                nc.tensor.transpose(x_turned[0, g, i][:, u, :], words_of(x_wide[0], i, g, u), ident[:])
+
+        def scale_x_half(g, i):
+            scaled(0, g, P * i, P * (i + 1), x_turned[0, g, i])
+
+        def quantise(values, codes, planes, lo, hi):
+            nc.vector.quantize_mx(
+                out=codes[:, lo:hi, :].rearrange("p g n -> p (g n)").bitcast(FP8X4),
+                scales=planes[:, lo:hi, :].rearrange("p g n -> p (g n)"),
+                in_=values[:, lo:hi, :, :].rearrange("p g n t -> p (g n t)"),
+            )
+
+        def quantise_x(c):
+            codes = work.tile([P, G, CH], U32, name="x_codes", align_bytes=64)
+            planes = work.tile([P, G, CH], U8, name="x_planes", align_bytes=64)
+            quantise(x_scaled[c], codes, planes, 0, G)
+            x_mx[c] = (codes, planes)
 
         def sort_r(c, i):
-            if c not in rs:
-                rs[c] = work.tile([P, 2, G, 2, P], F32, name="rsort")
+            if c not in r_sorted:
+                r_sorted[c] = work.tile([P, HALVES, G, 2, P], F32, name="r_sorted")
             nc.scalar.copy(
-                out=rs[c][:, i, :, :, :],
-                in_=rt[c][:, i, :].bitcast(F32).rearrange("p (h m u) -> p h u m", h=G, u=2),
+                out=r_sorted[c][:, i, :, :, :],
+                in_=r_raw[c][:, i, :].bitcast(F32).rearrange("p (h m u) -> p h u m", h=G, u=2),
             )
 
         def turn_r(c, h):
-            rp[c, h] = pst.tile([P, 2, CH], F32, name="rp" + str(h))
-            for i in range(2):
+            r_turned[c, h] = turned.tile([P, CH // RUN, 2, RUN], F32, name="r_turned" + str(h))
+            runs = P // RUN
+            for i in range(HALVES):
                 for u in range(2):
-                    if c not in rs:
-                        words = rt[c][:, i, :].bitcast(F32)[:, 256 * h + u : 256 * (h + 1) : 2]
-                    else:
-                        words = rs[c][:, i, h, u, :]
-                    nc.tensor.transpose(rp[c, h][:, u, i * P : (i + 1) * P], words, ident[:])
+                    words = r_sorted[c][:, i, h, u, :] if c in r_sorted else words_of(r_raw[c], i, h, u)
+                    nc.tensor.transpose(r_turned[c, h][:, runs * i : runs * (i + 1), u, :], words, ident[:])
 
-        def halves(bank):
-            return bank[:].rearrange("p u n -> p (u n)").bitcast(BF16).rearrange("p (u n e) -> p n u e", u=2, e=2)
-
-        def product(c, g):
-            if c not in xg:
-                xg[c] = work.tile([P, G, CH, 4], BF16, name="xg", align_bytes=64)
-            nc.vector.tensor_tensor(
-                out=xg[c][:, g, :, :].rearrange("p n (u e) -> p n u e", u=2),
-                in0=halves(xt[c, g]),
-                in1=sx[:, g, :].unsqueeze(1).to_broadcast([P, CH, 4]).rearrange("p n (u e) -> p n u e", u=2),
-                op=ALU.mult,
-            )
-
-        def product_first(g, i):
-            if 0 not in xg:
-                xg[0] = work.tile([P, G, CH, 4], BF16, name="xg", align_bytes=64)
-            nc.vector.tensor_tensor(
-                out=xg[0][:, g, i * P : (i + 1) * P, :].rearrange("p n (u e) -> p n u e", u=2),
-                in0=halves(xt[0, g, i]),
-                in1=sx[:, g, :].unsqueeze(1).to_broadcast([P, P, 4]).rearrange("p n (u e) -> p n u e", u=2),
-                op=ALU.mult,
-            )
-
-        def quantise(src, dst, lo, hi):
-            nc.vector.quantize_mx(
-                out=dst[0][:, lo:hi, :].rearrange("p g n -> p (g n)").bitcast(FP8X4),
-                scales=dst[1][:, lo:hi, :].rearrange("p g n -> p (g n)"),
-                in_=src[:, lo:hi, :, :].rearrange("p g n t -> p (g n t)"),
-            )
-
-        def quant_x(c, lo, hi):
-            if lo == 0:
-                xc[c] = (
-                    work.tile([P, G, CH], U32, name="xcodes", align_bytes=64),
-                    work.tile([P, G, CH], U8, name="xcs", align_bytes=64),
-                )
-            quantise(xg[c], xc[c], lo, hi)
-
-        def stage1(c, h, b):
-            q = psq.tile([P, 2, CH], F32, name="acc")
-            acc1[c, h, b] = q
-            for tt in range(2):
-                t = 2 * b + tt
-                cols = slice(512 * h + P * t, 512 * h + P * (t + 1))
+        def project(c, h, b):
+            codes, planes = x_mx[c]
+            q_sums[c, h, b] = sums.tile([P, 2, CH], F32, name="bank")
+            for k in range(2):
+                first = P * PACK * h + P * (2 * b + k)
+                cols = slice(first, first + P)
                 for g in range(G):
                     nc.tensor.matmul_mx(
-                        out=q[:, tt, :],
-                        lhsT=w_per[:, g, cols].bitcast(FP8X4),
-                        lhsT_scale=ws_per[4 * g :, cols],
-                        rhs=xc[c][0][:, g, :].bitcast(FP8X4),
-                        rhs_scale=xc[c][1][:, g, :],
+                        out=q_sums[c, h, b][:, k, :],
+                        lhsT=wq_sorted[:, g, cols].bitcast(FP8X4),
+                        lhsT_scale=wq_planes_sorted[4 * g :, cols],
+                        rhs=codes[:, g, :].bitcast(FP8X4),
+                        rhs_scale=planes[:, g, :],
                         start=(g == 0),
                         stop=(g == G - 1),
                     )
 
         def sigmoid(c, h, b):
-            if (c, h) not in sg:
-                sg[c, h] = work.tile([P, 4, CH], F32, name="sig" + str(h), align_bytes=64)
-            for tt in range(2):
-                t = 2 * b + tt
+            if (c, h) not in sig:
+                sig[c, h] = work.tile([P, CH // RUN, PACK, RUN], F32, name="sig" + str(h), align_bytes=64)
+            for k in range(2):
+                t = 2 * b + k
                 nc.scalar.activation(
-                    out=sg[c, h][:, t, :], in_=acc1[c, h, b][:, tt, :], func=ACT.Sigmoid, bias=bq[:, h, t : t + 1]
+                    out=sig[c, h][:, :, t, :],
+                    in_=q_sums[c, h, b][:, k, :].rearrange("p (m i) -> p m i", i=RUN),
+                    func=ACT.Sigmoid,
+                    bias=wq_bias[:, h, t : t + 1],
                 )
 
         def gate(c, h):
-            if c not in yg:
-                yg[c] = work.tile([P, G, CH, 4], BF16, name="yg", align_bytes=64)
+            if c not in y:
+                y[c] = work.tile([P, G, CH, PACK], BF16, name="y", align_bytes=64)
             nc.vector.tensor_tensor(
-                out=yg[c][:, h, :, :].rearrange("p n (u e) -> p n u e", u=2),
-                in0=sg[c, h][:].rearrange("p (u e) n -> p n u e", u=2),
-                in1=halves(rp[c, h]),
+                out=y[c][:, h, :, :].rearrange("p (m i) (u e) -> p m u e i", i=RUN, u=2),
+                in0=sig[c, h][:].rearrange("p m (u e) i -> p m u e i", u=2),
+                in1=r_turned[c, h][:].bitcast(BF16).rearrange("p m u (i e) -> p m u e i", e=2),
                 op=ALU.mult,
             )
 
-        def quant_y(c, lo, hi):
-            if c not in yc:
-                yc[c] = (
-                    work.tile([P, G, CH], U32, name="ycodes", align_bytes=64),
-                    work.tile([P, G, CH], U8, name="ycs", align_bytes=64),
-                )
-            quantise(yg[c], yc[c], lo, hi)
+        def quantise_y(c, lo, hi):
+            if c not in y_mx:
+                codes = work.tile([P, G, CH], U32, name="y_codes", align_bytes=64)
+                planes = work.tile([P, G, CH], U8, name="y_planes", align_bytes=64)
+                y_mx[c] = (codes, planes)
+            quantise(y[c], y_mx[c][0], y_mx[c][1], lo, hi)
 
-        def stage2(c, b, hs=(0, 1)):
-            i, d = b // 2, b % 2
-            if hs[0] == 0:
-                acc[c, b] = psq.tile([P, 512], F32, name="acc")
-            cols = slice(512 * d, 512 * (d + 1))
-            toks = slice(P * i, P * (i + 1))
-            for h in hs:
+        def block(b):
+            return b // 2, slice(N_OUT * (b % 2), N_OUT * (b % 2 + 1))
+
+        def contract(c, b, lo, hi):
+            i, cols = block(b)
+            codes, planes = y_mx[c]
+            tokens = slice(P * i, P * (i + 1))
+            if lo == 0:
+                out_sums[c, b] = sums.tile([P, N_OUT], F32, name="bank")
+            for h in range(lo, hi):
                 nc.tensor.matmul_mx(
-                    out=acc[c, b][:],
-                    lhsT=yc[c][0][:, h, toks].bitcast(FP8X4),
-                    lhsT_scale=yc[c][1][:, h, toks],
-                    rhs=w_out[:, h, cols].bitcast(FP8X4),
-                    rhs_scale=ws_out[4 * h :, cols],
+                    out=out_sums[c, b][:],
+                    lhsT=codes[:, h, tokens].bitcast(FP8X4),
+                    lhsT_scale=planes[:, h, tokens],
+                    rhs=out_words[:, h, cols].bitcast(FP8X4),
+                    rhs_scale=out_planes[4 * h :, cols],
                     start=(h == 0),
                     stop=(h == G - 1),
                 )
 
-        def finish(c, b, how="v"):
-            i, d = b // 2, b % 2
-            cols = slice(512 * d, 512 * (d + 1))
-            if (c, i) not in ob:
-                ob[c, i] = work.tile([P, D], F32, name="ob", bufs=8)
-            if how == "v":
-                nc.vector.tensor_tensor(out=ob[c, i][:, cols], in0=acc[c, b][:], in1=b2[:, cols], op=ALU.add)
-            elif how == "s":
-                raw[c, b] = work.tile([P, 512], F32, name="raw")
-                nc.scalar.copy(out=raw[c, b][:], in_=acc[c, b][:])
-                return
-            else:
-                nc.gpsimd.tensor_tensor(out=ob[c, i][:, cols], in0=raw[c, b][:], in1=b2[:, cols], op=ALU.add)
-            nc.sync.dma_start(out=o_view[:, 2 * c + i, cols], in_=ob[c, i][:, cols])
+        def stash(c, b):
+            stashed[c, b] = work.tile([P, N_OUT], F32, name="stashed")
+            nc.scalar.copy(out=stashed[c, b][:], in_=out_sums[c, b][:])
 
-        def permute(g):
-            nc.vector.tensor_copy(
-                out=w_per[:, g, :].rearrange("p (h t m) -> p h t m", h=2, t=4),
-                in_=w_raw[:, g, :].rearrange("p (h m t) -> p h t m", h=2, t=4),
-            )
+        def finish(engine, summed, c, b):
+            i, cols = block(b)
+            if (c, i) not in result:
+                result[c, i] = work.tile([P, D], F32, name="result", bufs=CHUNKS * HALVES)
+            engine.tensor_tensor(out=result[c, i][:, cols], in0=summed[:], in1=out_bias[:, cols], op=ALU.add)
+            nc.sync.dma_start(out=out_rows[:, HALVES * c + i, cols], in_=result[c, i][:, cols])
 
-        def permute_scales(eng):
-            (nc.vector if eng == "V" else nc.gpsimd).tensor_copy(
-                out=ws_per[:].rearrange("p (h t m) -> p h t m", h=2, t=4),
-                in_=ws_raw[:].rearrange("p (h m t) -> p h t m", h=2, t=4),
-            )
+        def add_bias(c, b):
+            finish(nc.vector, out_sums[c, b], c, b)
 
-        widen(0, 0, "v", 512, 1024)
-        widen(0, 0, "s", 0, 512)
-        widen(0, 1, "v", 512, 1024)
-        widen(0, 1, "s", 0, 512)
-        turn_first(1, 0)
-        turn_first(1, 1)
-        turn_first(0, 0)
-        permute(0)
-        turn_first(0, 1)
-        widen(1, 1, "s")
-        product_first(1, 1)
-        permute_scales("G")
-        product_first(0, 0)
-        widen(1, 0, "s")
-        product_first(1, 0)
-        product_first(0, 1)
-        permute(1)
+        def add_bias_stashed(c, b):
+            finish(nc.gpsimd, stashed[c, b], c, b)
+
+        load_x(0, 0, 1)
+        load_x(0, 1, 2)
+        load_words(wq_words, wq_w_words, 0)
+        load_x(1, 0, 2)
+        load_scales(wq_planes, wq_w_scales)
+        load_words(wq_words, wq_w_words, 1)
+        nc.sync.dma_start(out=wq_bias[:], in_=wq_b.rearrange("(h p t) -> p h t", p=P, t=PACK))
+        load_r(0)
+        load_x(2, 0, 2)
+        load_scales(out_planes, out_w_scales)
+        load_words(out_words, out_w_words, 0)
+        load_words(out_words, out_w_words, 1)
+        load_x(3, 0, 2)
+        load_r(1)
+        load_r(2)
+        load_r(3)
+        nc.sync.dma_start(out=out_bias[:], in_=out_b.partition_broadcast(P))
+
+        widen(nc.vector.tensor_copy, 0, 0, slice(512, 1024))
+        widen(nc.scalar.copy, 0, 0, slice(0, 512))
+        widen(nc.vector.tensor_copy, 0, 1, slice(512, 1024))
+        widen(nc.scalar.copy, 0, 1, slice(0, 512))
+        turn_x_half(1, 0)
+        turn_x_half(0, 0)
+        turn_x_half(1, 1)
+        permute_words(0)
+        turn_x_half(0, 1)
+        widen(nc.scalar.copy, 1, 0, slice(0, D))
+        scale_x_half(1, 1)
+        permute_scales(nc.gpsimd)
+        scale_x_half(1, 0)
+        widen(nc.scalar.copy, 1, 1, slice(0, D))
+        scale_x_half(0, 0)
+        scale_x_half(0, 1)
+        permute_words(1)
         turn_x(1, 0)
-        quant_x(0, 0, 2)
-        widen(2, 0, "s")
+        quantise_x(0)
+        widen(nc.scalar.copy, 2, 1, slice(0, D))
         turn_x(1, 1)
-        product(1, 0)
-        stage1(0, 0, 1)
-        widen(2, 1, "s")
-        stage1(0, 0, 0)
-        product(1, 1)
-        turn_r(0, 0)
-        sigmoid(0, 0, 0)
-        turn_x(2, 0)
-        sigmoid(0, 0, 1)
-        quant_x(1, 0, 2)
-        turn_x(2, 1)
-        widen(3, 1, "s")
-        product(2, 0)
-        turn_r(0, 1)
-        stage1(0, 1, 1)
-        widen(3, 0, "s")
-        product(2, 1)
-        stage1(0, 1, 0)
-        stage1(1, 0, 0)
+        scale_x(1, 0)
+        project(0, 1, 1)
+        widen(nc.scalar.copy, 2, 0, slice(0, D))
+        project(0, 0, 0)
+        scale_x(1, 1)
+        project(0, 1, 0)
         sigmoid(0, 1, 1)
-        gate(0, 0)
-        stage1(1, 1, 1)
+        turn_x(2, 0)
+        sigmoid(0, 0, 0)
+        quantise_x(1)
+        turn_r(0, 1)
         sigmoid(0, 1, 0)
-        stage1(1, 1, 0)
+        scale_x(2, 0)
+        turn_x(2, 1)
+        sort_r(1, 1)
+        turn_r(0, 0)
+        sort_r(1, 0)
+        scale_x(2, 1)
+        project(0, 0, 1)
+        widen(nc.scalar.copy, 3, 1, slice(0, D))
+        project(1, 1, 1)
+        gate(0, 1)
+        project(1, 0, 0)
+        sigmoid(0, 0, 1)
+        project(1, 1, 0)
+        widen(nc.scalar.copy, 3, 0, slice(0, D))
+        gate(0, 0)
+        project(1, 0, 1)
         sort_r(2, 0)
-        quant_x(2, 0, 2)
+        turn_r(1, 1)
+        quantise_x(2)
+        turn_x(3, 1)
+        sigmoid(1, 1, 1)
+        quantise_y(0, 0, G)
+        turn_r(1, 0)
         sigmoid(1, 0, 0)
         turn_x(3, 0)
-        gate(0, 1)
+        scale_x(3, 1)
         sigmoid(1, 1, 0)
-        turn_x(3, 1)
-        sort_r(2, 1)
-        turn_r(1, 0)
-        product(3, 0)
-        sigmoid(1, 1, 1)
-        turn_r(1, 1)
-        sort_r(3, 1)
-        stage1(2, 0, 1)
-        quant_y(0, 0, 2)
-        sort_r(3, 0)
-        stage1(2, 0, 0)
-        product(3, 1)
-        sigmoid(2, 0, 1)
-        stage1(1, 0, 1)
-        sigmoid(2, 0, 0)
-        stage1(2, 1, 1)
-        gate(1, 1)
+        project(2, 1, 0)
         sigmoid(1, 0, 1)
-        stage1(2, 1, 0)
-        sigmoid(2, 1, 1)
-        stage2(0, 2)
-        quant_x(3, 0, 2)
+        contract(0, 2, 0, G)
+        scale_x(3, 0)
         sigmoid(2, 1, 0)
+        contract(0, 3, 0, G)
+        stash(0, 2)
         gate(1, 0)
-        turn_r(2, 1)
-        stage1(3, 1, 0)
-        stage1(3, 0, 0)
-        gate(2, 1)
-        sigmoid(3, 1, 0)
-        stage1(3, 1, 1)
-        finish(0, 2, "s")
-        quant_y(1, 0, 2)
+        project(2, 0, 1)
+        stash(0, 3)
+        project(2, 1, 1)
+        add_bias_stashed(0, 2)
+        sort_r(2, 1)
+        gate(1, 1)
+        project(2, 0, 0)
+        sigmoid(2, 0, 1)
+        contract(0, 0, 0, G)
+        sigmoid(2, 0, 0)
+        quantise_x(3)
         turn_r(2, 0)
+        sigmoid(2, 1, 1)
+        turn_r(2, 1)
+        quantise_y(1, 0, G)
+        sort_r(3, 1)
+        project(3, 1, 1)
+        add_bias(0, 0)
+        contract(1, 1, 0, G)
+        gate(2, 1)
         sigmoid(3, 1, 1)
-        turn_r(3, 1)
-        finish(0, 2, "g")
+        project(3, 1, 0)
+        stash(1, 1)
+        contract(1, 0, 0, G)
         gate(2, 0)
+        sigmoid(3, 1, 0)
+        contract(1, 3, 0, G)
+        add_bias_stashed(1, 1)
+        sort_r(3, 0)
+        project(3, 0, 0)
+        add_bias(1, 0)
+        stash(1, 3)
+        project(3, 0, 1)
+        quantise_y(2, 0, G)
         sigmoid(3, 0, 0)
-        stage2(1, 2)
-        stage2(0, 3)
-        gate(3, 1)
-        finish(1, 2, "s")
-        stage2(0, 0)
-        finish(0, 3, "s")
-        stage2(1, 3)
-        finish(1, 2, "g")
-        finish(0, 0, "v")
-        stage1(3, 0, 1)
-        quant_y(3, 1, 2)
-        finish(1, 3, "s")
-        stage2(1, 0)
-        quant_y(2, 0, 2)
+        turn_r(3, 1)
+        add_bias_stashed(1, 3)
         sigmoid(3, 0, 1)
         turn_r(3, 0)
-        finish(1, 3, "g")
-        finish(1, 0, "v")
-        stage2(2, 1)
+        gate(3, 1)
+        contract(1, 2, 0, G)
+        add_bias_stashed(0, 3)
+        contract(2, 2, 0, G)
+        stash(1, 2)
         gate(3, 0)
-        stage2(2, 2)
-        finish(0, 3, "g")
-        stage2(1, 1)
-        finish(2, 1, "v")
-        finish(2, 2, "s")
-        stage2(2, 3)
-        quant_y(3, 0, 1)
-        finish(1, 1, "v")
-        finish(2, 2, "g")
-        stage2(2, 0)
-        finish(2, 3, "s")
-        stage2(3, 3, (0,))
-        stage2(3, 3, (1,))
-        finish(2, 0, "v")
-        stage2(3, 0, (0,))
-        finish(2, 3, "g")
-        stage2(3, 2, (0,))
-        finish(3, 3, "v")
-        stage2(3, 0, (1,))
-        stage2(3, 2, (1,))
-        stage2(3, 1, (0,))
-        finish(3, 0, "s")
-        stage2(3, 1, (1,))
-        finish(3, 2, "v")
-        stage2(0, 1)
-        finish(3, 1, "v")
-        finish(3, 0, "g")
-        finish(0, 1, "v")
+        contract(2, 1, 0, G)
+        stash(2, 2)
+        contract(2, 0, 0, G)
+        add_bias_stashed(1, 2)
+        add_bias(2, 1)
+        contract(2, 3, 0, G)
+        quantise_y(3, 0, 1)
+        contract(0, 1, 0, G)
+        add_bias(2, 0)
+        add_bias_stashed(2, 2)
+        stash(2, 3)
+        contract(3, 1, 0, 1)
+        quantise_y(3, 1, 2)
+        add_bias(0, 1)
+        contract(3, 3, 0, 1)
+        contract(3, 1, 1, G)
+        add_bias_stashed(2, 3)
+        contract(3, 0, 0, 1)
+        contract(3, 0, 1, G)
+        add_bias(3, 1)
+        contract(3, 3, 1, G)
+        contract(3, 2, 0, 1)
+        stash(3, 0)
+        contract(3, 2, 1, G)
+        add_bias(3, 3)
+        add_bias(3, 2)
+        add_bias_stashed(3, 0)

from contextlib import ExitStack

import concourse.mybir as mybir
from concourse.masks import make_identity

F32 = mybir.dt.float32
BF16 = mybir.dt.bfloat16
I32 = mybir.dt.int32
U32 = mybir.dt.uint32
U8 = mybir.dt.uint8
FP8 = mybir.dt.float8_e4m3fn
FP8X4 = mybir.dt.float8_e4m3fn_x4
ACT = mybir.ActivationFunctionType
ALU = mybir.AluOpType

S, D = 1024, 1024
P = 128
PACK = 4
G = D // (P * PACK)
CHUNKS = 4
CH = S // CHUNKS
HALVES = CH // P
RUN = 4
N_OUT = 512

FLOPS = 2 * 2 * S * D * D


def tile_aft_full_pb_w8_kernel(
    tc, x_bytes, x_scale, wq_w_words, wq_w_scales, wq_b, r_aft, out_w_words, out_w_scales, out_b, out
):
    nc = tc.nc
    with ExitStack() as ctx:
        const = ctx.enter_context(tc.tile_pool(name="const", bufs=1))
        work = ctx.enter_context(tc.tile_pool(name="work", bufs=CHUNKS))
        turned = ctx.enter_context(tc.psum_pool(name="turned", bufs=1))
        sums = ctx.enter_context(tc.psum_pool(name="sums", bufs=4))
        ctx.enter_context(tc.manual_schedule())

        x_rows = x_bytes.rearrange("o (p j) k -> p (o j) k", j=CHUNKS * HALVES)
        r_rows = r_aft.rearrange("o (p j) k -> p (o j) k", j=CHUNKS * HALVES)
        out_rows = out.rearrange("o (p j) k -> p (o j) k", j=CHUNKS * HALVES)

        ident = const.tile([P, P], F32, name="ident")
        warm = const.tile([P, 1], F32, name="warm")
        scale_x_by = const.tile([P, G, PACK], F32, name="scale_x_by")
        wq_bias = const.tile([P, G, PACK], BF16, name="wq_bias")
        out_bias = const.tile([P, D], BF16, name="out_bias")
        wq_words = const.tile([P, G, D], I32, name="wq_words", align_bytes=64)
        wq_sorted = const.tile([P, G, D], I32, name="wq_sorted", align_bytes=64)
        out_words = const.tile([P, G, D], I32, name="out_words", align_bytes=64)
        wq_planes = const.tile([P, D], U8, name="wq_planes", align_bytes=64)
        wq_planes_sorted = const.tile([P, D], U8, name="wq_planes_sorted", align_bytes=64)
        out_planes = const.tile([P, D], U8, name="out_planes", align_bytes=64)

        nc.gpsimd.memset(warm[:], 0.0)
        make_identity(nc, ident[:])
        nc.vector.memset(wq_planes[:].bitcast(I32), 0)
        nc.vector.memset(out_planes[:].bitcast(I32), 0)
        nc.scalar.dma_start(out=scale_x_by[:], in_=x_scale.rearrange("o s (g p t) -> p (o s g) t", p=P, t=PACK))
        nc.scalar.activation(out=warm[:], in_=warm[:], func=ACT.Sigmoid)

        x_raw, x_wide, x_turned, x_scaled, x_mx = {}, {}, {}, {}, {}
        r_raw, r_sorted, r_turned = {}, {}, {}
        q_sums, sig, y, y_mx = {}, {}, {}, {}
        out_sums, stashed, result = {}, {}, {}

        def load_x(c, lo, hi):
            if c not in x_raw:
                x_raw[c] = work.tile([P, HALVES, D], U8, name="x_raw")
            nc.sync.dma_start(out=x_raw[c][:, lo:hi, :], in_=x_rows[:, HALVES * c + lo : HALVES * c + hi, :])

        def load_r(c):
            r_raw[c] = work.tile([P, HALVES, D], BF16, name="r_raw")
            nc.sync.dma_start(out=r_raw[c][:], in_=r_rows[:, HALVES * c : HALVES * (c + 1), :])

        def load_words(words, source, g):
            nc.sync.dma_start(out=words[:, g, :], in_=source[g].rearrange("p n t -> p (n t)").bitcast(I32))

        def load_scales(planes, source):
            for quad in range(4):
                nc.sync.dma_start(
                    out=planes[32 * quad : 32 * quad + 4 * G, :].bitcast(I32),
                    in_=source[:, 4 * quad : 4 * quad + 4, :].bitcast(I32),
                )

        def permute_words(g):
            nc.vector.tensor_copy(
                out=wq_sorted[:, g, :].rearrange("p (h t m) -> p h m t", h=G, t=PACK),
                in_=wq_words[:, g, :].rearrange("p (h m t) -> p h m t", h=G, t=PACK),
            )

        def permute_scales(engine):
            engine.tensor_copy(
                out=wq_planes_sorted[:].rearrange("p (h t m) -> p h t m", h=G, t=PACK),
                in_=wq_planes[:].rearrange("p (h m t) -> p h t m", h=G, t=PACK),
            )

        def widen(copy, c, i, cols):
            if c not in x_wide:
                x_wide[c] = work.tile([P, HALVES, D], BF16, name="x_wide")
            copy(out=x_wide[c][:, i, cols], in_=x_raw[c][:, i, cols].bitcast(FP8))

        def words_of(row_tile, i, group, u):
            return row_tile[:, i, :].bitcast(F32)[:, 256 * group + u : 256 * (group + 1) : 2]

        def slots_of(bank):
            return bank[:].rearrange("p u n -> p (u n)").bitcast(BF16).rearrange("p (u n e) -> p n u e", u=2, e=2)

        def turn_x(c, g):
            x_turned[c, g] = turned.tile([P, 2, CH], F32, name="x_turned" + str(g))
            for i in range(HALVES):
                for u in range(2):
                    nc.tensor.transpose(
                        x_turned[c, g][:, u, P * i : P * (i + 1)], words_of(x_wide[c], i, g, u), ident[:]
                    )

        def scaled(c, g, lo, hi, bank):
            if c not in x_scaled:
                x_scaled[c] = work.tile([P, G, CH, PACK], BF16, name="x_scaled", align_bytes=64)
            by = scale_x_by[:, g, :].unsqueeze(1).to_broadcast([P, hi - lo, PACK])
            nc.vector.tensor_tensor(
                out=x_scaled[c][:, g, lo:hi, :].rearrange("p n (u e) -> p n u e", u=2),
                in0=slots_of(bank),
                in1=by.rearrange("p n (u e) -> p n u e", u=2),
                op=ALU.mult,
            )

        def scale_x(c, g):
            scaled(c, g, 0, CH, x_turned[c, g])

        def turn_x_half(g, i):
            if i == 0:
                x_turned[0, g, i] = turned.tile([P, 2, P], F32, name="x_turned" + str(g))
            else:
                x_turned[0, g, i] = sums.tile([P, 2, P], F32, name="bank")
            for u in range(2):
                nc.tensor.transpose(x_turned[0, g, i][:, u, :], words_of(x_wide[0], i, g, u), ident[:])

        def scale_x_half(g, i):
            scaled(0, g, P * i, P * (i + 1), x_turned[0, g, i])

        def quantise(values, codes, planes, lo, hi):
            nc.vector.quantize_mx(
                out=codes[:, lo:hi, :].rearrange("p g n -> p (g n)").bitcast(FP8X4),
                scales=planes[:, lo:hi, :].rearrange("p g n -> p (g n)"),
                in_=values[:, lo:hi, :, :].rearrange("p g n t -> p (g n t)"),
            )

        def quantise_x(c):
            codes = work.tile([P, G, CH], U32, name="x_codes", align_bytes=64)
            planes = work.tile([P, G, CH], U8, name="x_planes", align_bytes=64)
            quantise(x_scaled[c], codes, planes, 0, G)
            x_mx[c] = (codes, planes)

        def sort_r(c, i):
            if c not in r_sorted:
                r_sorted[c] = work.tile([P, HALVES, G, 2, P], F32, name="r_sorted")
            nc.scalar.copy(
                out=r_sorted[c][:, i, :, :, :],
                in_=r_raw[c][:, i, :].bitcast(F32).rearrange("p (h m u) -> p h u m", h=G, u=2),
            )

        def turn_r(c, h):
            r_turned[c, h] = turned.tile([P, CH // RUN, 2, RUN], F32, name="r_turned" + str(h))
            runs = P // RUN
            for i in range(HALVES):
                for u in range(2):
                    words = r_sorted[c][:, i, h, u, :] if c in r_sorted else words_of(r_raw[c], i, h, u)
                    nc.tensor.transpose(r_turned[c, h][:, runs * i : runs * (i + 1), u, :], words, ident[:])

        def project(c, h, b):
            codes, planes = x_mx[c]
            q_sums[c, h, b] = sums.tile([P, 2, CH], F32, name="bank")
            for k in range(2):
                first = P * PACK * h + P * (2 * b + k)
                cols = slice(first, first + P)
                for g in range(G):
                    nc.tensor.matmul_mx(
                        out=q_sums[c, h, b][:, k, :],
                        lhsT=wq_sorted[:, g, cols].bitcast(FP8X4),
                        lhsT_scale=wq_planes_sorted[4 * g :, cols],
                        rhs=codes[:, g, :].bitcast(FP8X4),
                        rhs_scale=planes[:, g, :],
                        start=(g == 0),
                        stop=(g == G - 1),
                    )

        def sigmoid(c, h, b):
            if (c, h) not in sig:
                sig[c, h] = work.tile([P, CH // RUN, PACK, RUN], F32, name="sig" + str(h), align_bytes=64)
            for k in range(2):
                t = 2 * b + k
                nc.scalar.activation(
                    out=sig[c, h][:, :, t, :],
                    in_=q_sums[c, h, b][:, k, :].rearrange("p (m i) -> p m i", i=RUN),
                    func=ACT.Sigmoid,
                    bias=wq_bias[:, h, t : t + 1],
                )

        def gate(c, h):
            if c not in y:
                y[c] = work.tile([P, G, CH, PACK], BF16, name="y", align_bytes=64)
            nc.vector.tensor_tensor(
                out=y[c][:, h, :, :].rearrange("p (m i) (u e) -> p m u e i", i=RUN, u=2),
                in0=sig[c, h][:].rearrange("p m (u e) i -> p m u e i", u=2),
                in1=r_turned[c, h][:].bitcast(BF16).rearrange("p m u (i e) -> p m u e i", e=2),
                op=ALU.mult,
            )

        def quantise_y(c, lo, hi):
            if c not in y_mx:
                codes = work.tile([P, G, CH], U32, name="y_codes", align_bytes=64)
                planes = work.tile([P, G, CH], U8, name="y_planes", align_bytes=64)
                y_mx[c] = (codes, planes)
            quantise(y[c], y_mx[c][0], y_mx[c][1], lo, hi)

        def block(b):
            return b // 2, slice(N_OUT * (b % 2), N_OUT * (b % 2 + 1))

        def contract(c, b, lo, hi):
            i, cols = block(b)
            codes, planes = y_mx[c]
            tokens = slice(P * i, P * (i + 1))
            if lo == 0:
                out_sums[c, b] = sums.tile([P, N_OUT], F32, name="bank")
            for h in range(lo, hi):
                nc.tensor.matmul_mx(
                    out=out_sums[c, b][:],
                    lhsT=codes[:, h, tokens].bitcast(FP8X4),
                    lhsT_scale=planes[:, h, tokens],
                    rhs=out_words[:, h, cols].bitcast(FP8X4),
                    rhs_scale=out_planes[4 * h :, cols],
                    start=(h == 0),
                    stop=(h == G - 1),
                )

        def stash(c, b):
            stashed[c, b] = work.tile([P, N_OUT], F32, name="stashed")
            nc.scalar.copy(out=stashed[c, b][:], in_=out_sums[c, b][:])

        def finish(engine, summed, c, b):
            i, cols = block(b)
            if (c, i) not in result:
                result[c, i] = work.tile([P, D], F32, name="result", bufs=CHUNKS * HALVES)
            engine.tensor_tensor(out=result[c, i][:, cols], in0=summed[:], in1=out_bias[:, cols], op=ALU.add)
            nc.sync.dma_start(out=out_rows[:, HALVES * c + i, cols], in_=result[c, i][:, cols])

        def add_bias(c, b):
            finish(nc.vector, out_sums[c, b], c, b)

        def add_bias_stashed(c, b):
            finish(nc.gpsimd, stashed[c, b], c, b)

        load_x(0, 0, 1)
        load_x(0, 1, 2)
        load_words(wq_words, wq_w_words, 0)
        load_x(1, 0, 2)
        load_scales(wq_planes, wq_w_scales)
        load_words(wq_words, wq_w_words, 1)
        nc.sync.dma_start(out=wq_bias[:], in_=wq_b.rearrange("(h p t) -> p h t", p=P, t=PACK))
        load_r(0)
        load_x(2, 0, 2)
        load_scales(out_planes, out_w_scales)
        load_words(out_words, out_w_words, 0)
        load_words(out_words, out_w_words, 1)
        load_x(3, 0, 2)
        load_r(1)
        load_r(2)
        load_r(3)
        nc.sync.dma_start(out=out_bias[:], in_=out_b.partition_broadcast(P))

        widen(nc.vector.tensor_copy, 0, 0, slice(512, 1024))
        widen(nc.scalar.copy, 0, 0, slice(0, 512))
        widen(nc.vector.tensor_copy, 0, 1, slice(512, 1024))
        widen(nc.scalar.copy, 0, 1, slice(0, 512))
        turn_x_half(1, 0)
        turn_x_half(0, 0)
        turn_x_half(1, 1)
        permute_words(0)
        turn_x_half(0, 1)
        widen(nc.scalar.copy, 1, 0, slice(0, D))
        scale_x_half(1, 1)
        permute_scales(nc.gpsimd)
        scale_x_half(1, 0)
        widen(nc.scalar.copy, 1, 1, slice(0, D))
        scale_x_half(0, 0)
        scale_x_half(0, 1)
        permute_words(1)
        turn_x(1, 0)
        quantise_x(0)
        widen(nc.scalar.copy, 2, 1, slice(0, D))
        turn_x(1, 1)
        scale_x(1, 0)
        project(0, 1, 1)
        widen(nc.scalar.copy, 2, 0, slice(0, D))
        project(0, 0, 0)
        scale_x(1, 1)
        project(0, 1, 0)
        sigmoid(0, 1, 1)
        turn_x(2, 0)
        sigmoid(0, 0, 0)
        quantise_x(1)
        turn_r(0, 1)
        sigmoid(0, 1, 0)
        scale_x(2, 0)
        turn_x(2, 1)
        sort_r(1, 1)
        turn_r(0, 0)
        sort_r(1, 0)
        scale_x(2, 1)
        project(0, 0, 1)
        widen(nc.scalar.copy, 3, 1, slice(0, D))
        project(1, 1, 1)
        gate(0, 1)
        project(1, 0, 0)
        sigmoid(0, 0, 1)
        project(1, 1, 0)
        widen(nc.scalar.copy, 3, 0, slice(0, D))
        gate(0, 0)
        project(1, 0, 1)
        sort_r(2, 0)
        turn_r(1, 1)
        quantise_x(2)
        turn_x(3, 1)
        sigmoid(1, 1, 1)
        quantise_y(0, 0, G)
        turn_r(1, 0)
        sigmoid(1, 0, 0)
        turn_x(3, 0)
        scale_x(3, 1)
        sigmoid(1, 1, 0)
        project(2, 1, 0)
        sigmoid(1, 0, 1)
        contract(0, 2, 0, G)
        scale_x(3, 0)
        sigmoid(2, 1, 0)
        contract(0, 3, 0, G)
        stash(0, 2)
        gate(1, 0)
        project(2, 0, 1)
        stash(0, 3)
        project(2, 1, 1)
        add_bias_stashed(0, 2)
        sort_r(2, 1)
        gate(1, 1)
        project(2, 0, 0)
        sigmoid(2, 0, 1)
        contract(0, 0, 0, G)
        sigmoid(2, 0, 0)
        quantise_x(3)
        turn_r(2, 0)
        sigmoid(2, 1, 1)
        turn_r(2, 1)
        quantise_y(1, 0, G)
        sort_r(3, 1)
        project(3, 1, 1)
        add_bias(0, 0)
        contract(1, 1, 0, G)
        gate(2, 1)
        sigmoid(3, 1, 1)
        project(3, 1, 0)
        stash(1, 1)
        contract(1, 0, 0, G)
        gate(2, 0)
        sigmoid(3, 1, 0)
        contract(1, 3, 0, G)
        add_bias_stashed(1, 1)
        sort_r(3, 0)
        project(3, 0, 0)
        add_bias(1, 0)
        stash(1, 3)
        project(3, 0, 1)
        quantise_y(2, 0, G)
        sigmoid(3, 0, 0)
        turn_r(3, 1)
        add_bias_stashed(1, 3)
        sigmoid(3, 0, 1)
        turn_r(3, 0)
        gate(3, 1)
        contract(1, 2, 0, G)
        add_bias_stashed(0, 3)
        contract(2, 2, 0, G)
        stash(1, 2)
        gate(3, 0)
        contract(2, 1, 0, G)
        stash(2, 2)
        contract(2, 0, 0, G)
        add_bias_stashed(1, 2)
        add_bias(2, 1)
        contract(2, 3, 0, G)
        quantise_y(3, 0, 1)
        contract(0, 1, 0, G)
        add_bias(2, 0)
        add_bias_stashed(2, 2)
        stash(2, 3)
        contract(3, 1, 0, 1)
        quantise_y(3, 1, 2)
        add_bias(0, 1)
        contract(3, 3, 0, 1)
        contract(3, 1, 1, G)
        add_bias_stashed(2, 3)
        contract(3, 0, 0, 1)
        contract(3, 0, 1, G)
        add_bias(3, 1)
        contract(3, 3, 1, G)
        contract(3, 2, 0, 1)
        stash(3, 0)
        contract(3, 2, 1, G)
        add_bias(3, 3)
        add_bias(3, 2)
        add_bias_stashed(3, 0)
